import numpy as np
import ml_dtypes


def mxq(x, axis, fmt="e4m3"):
    dtype, down = {"e4m3": (ml_dtypes.float8_e4m3fn, 7), "e5m2": (ml_dtypes.float8_e5m2, 14)}[fmt]
    v = np.moveaxis(np.asarray(x, np.float32).astype(ml_dtypes.bfloat16).astype(np.float64), axis, -1)
    blocks = v.reshape(v.shape[:-1] + (-1, 32))
    amax = np.abs(blocks).max(-1, keepdims=True)
    byte = np.maximum(np.where(amax > 0, np.frexp(amax)[1] - 1 + 127, 0) - down, 1)
    scale = np.exp2(byte - 127.0)
    codes = (blocks / scale).astype(np.float32).astype(dtype).astype(np.float64)
    return np.moveaxis((codes * scale).reshape(v.shape), -1, axis)


WIDE = False


def mx_kscale(k):
    if not WIDE:
        return np.ones(k)
    levels = np.array([10, -10, 5, -5, 0])
    if k % 512:
        return np.exp2(np.random.permutation(np.resize(levels, k // 32))).repeat(32)
    a = np.empty((k // 512, 16))
    for p in range(k // 512):
        a[p, :8] = np.random.permutation(np.resize(levels, 8))
        for g in range(8):
            far = levels[np.abs(levels - a[p, g]) >= 10]
            a[p, g + 8] = far[np.random.randint(len(far))]
    return np.exp2(a.ravel()).repeat(32)


BF16 = ml_dtypes.bfloat16


def bf(x):
    return np.asarray(x, np.float32).astype(BF16)


def f64(x):
    return np.asarray(x).astype(np.float64)


B, D, U = 8192, 2048, 512
MASK_DENSITY = 1.0 / 16.0
W_STD = 1.0 / np.sqrt(U * MASK_DENSITY)


def setup_inputs():
    s, t = mx_kscale(U), mx_kscale(U)
    return {"h0": bf(np.random.standard_normal((B, U)) * s),
            "k1": bf(np.random.standard_normal((U, U)) * W_STD / s[:, None] * t),
            "k2": bf(np.random.standard_normal((U, U)) * W_STD / t[:, None]),
            "m1": bf(np.random.random((U, U)) < MASK_DENSITY),
            "m2": bf(np.random.random((U, U)) < MASK_DENSITY),
            "scaling": bf(np.random.uniform(1.25, 1.75, 1)),
            "bias": bf(np.random.standard_normal(U) * 0.5)}


def reference(h0, k1, k2, m1, m2, scaling, bias):
    w1 = f64(k1) * f64(m1)
    w2 = f64(k2) * f64(m2)
    h1 = mxq(f64(h0), 1, "e4m3") @ mxq(w1, 0, "e4m3")
    out = mxq(h1, 1, "e4m3") @ mxq(w2, 0, "e4m3")
    return np.maximum(f64(scaling) * out + f64(bias), 0.0)

@@ -1,0 +1,346 @@
+from contextlib import ExitStack
+
+import concourse.masks as masks
+import concourse.mybir as mybir
+
+F32 = mybir.dt.float32
+BF16 = mybir.dt.bfloat16
+U32 = mybir.dt.uint32
+U8 = mybir.dt.uint8
+FP8X4 = mybir.dt.float8_e4m3fn_x4
+ALU = mybir.AluOpType
+ACT = mybir.ActivationFunctionType
+
+P = 128
+ROWS = 8192
+U = 512
+TILES = ROWS // P
+GROUP = 4
+NG = TILES // GROUP
+GCOLS = GROUP * P
+FLT_MAX = 3.4028234663852886e38
+PAD = 8
+STORE_TILES = 2
+S_COLS = 256
+FLOPS = 2 * 2 * ROWS * U * U
+
+CHUNKS = [1, 1, 2, 4, 4, 4]
+LAG_A = 3
+LAG_C = 2
+LAG_G = 2
+MANUAL = True
+OFF = 0
+NK = NG + (1 if OFF else 0)
+Y_BUFS = 6
+
+
+def pattern(k):
+    return "SSSS" if k >= 12 else "TTTT"
+
+
+def per_tile(k):
+    return k >= 12
+
+
+def e_engine(g, jj):
+    return "S"
+
+
+def b_engine(g, h):
+    return "S"
+
+
+def f_split(g):
+    return 1
+
+
+def tile_sparsefactorisationdense_pa_t_kernel(tc, h0, k1, k2, m1, m2, scaling, bias, out):
+    nc = tc.nc
+    with ExitStack() as ctx:
+        const = ctx.enter_context(tc.tile_pool(name="const", bufs=1))
+        stage = ctx.enter_context(tc.tile_pool(name="stage", bufs=4))
+        quant = ctx.enter_context(tc.tile_pool(name="quant", bufs=5))
+        ypool = ctx.enter_context(tc.tile_pool(name="ypool", bufs=Y_BUFS))
+        tpool = ctx.enter_context(tc.psum_pool(name="tpool", bufs=2))
+        s1pool = ctx.enter_context(tc.psum_pool(name="s1pool", bufs=3))
+        s2pool = ctx.enter_context(tc.psum_pool(name="s2pool", bufs=3))
+        if MANUAL:
+            ctx.enter_context(tc.manual_schedule())
+
+        h0v = h0.rearrange("(p j) k -> p (j k)", j=TILES)
+        outv = out.rearrange("(p j) n -> p j n", j=TILES)
+
+        brow = const.tile([P, U + 64], BF16, name="brow")
+        ones = const.tile([P, P], BF16, name="ones")
+        nc.vector.memset(brow[:], 0.0)
+        nc.vector.memset(ones[:], 1.0)
+        warm = const.tile([P, 8], F32, name="warm")
+        nc.vector.memset(warm[:], 0.0)
+        nc.scalar.dma_start(out=brow[0:1, 0:U], in_=bias.rearrange("(o n) -> o n", o=1))
+        nc.scalar.dma_start(out=brow[0:1, U : U + 1], in_=scaling.rearrange("(o n) -> o n", o=1))
+        nc.scalar.activation(out=warm[:], in_=warm[:], func=ACT.Relu)
+        ident = const.tile([P, P], F32, name="ident")
+        masks.make_identity(nc, ident[:])
+
+        k1_sb = const.tile([P, 4 * U], BF16, name="k1_sb")
+        m1_sb = const.tile([P, 4 * U], BF16, name="m1_sb")
+        k2_sb = const.tile([P, 4 * U], BF16, name="k2_sb")
+        m2_sb = const.tile([P, 4 * U], BF16, name="m2_sb")
+
+        def load_w1(dst, src):
+            nc.sync.dma_start(out=dst[:], in_=src.rearrange("(p j) c -> p (j c)", j=4))
+
+        def load_w2(dst, src):
+            nc.sync.dma_start(out=dst[:], in_=src.rearrange("(p j) c -> p (j c)", j=4))
+
+        h0_tiles = []
+        group_src = []
+        g_first = 0
+        for c, n in enumerate(CHUNKS):
+            t = const.tile([P, n * GROUP * U], BF16, name="h0c%d" % c)
+            h0_tiles.append((t, g_first, n))
+            for i in range(n):
+                group_src.append((t, i))
+            g_first += n
+
+        def load_h0(c):
+            t, g_a, n = h0_tiles[c]
+            nc.sync.dma_start(out=t[:], in_=h0v[:, g_a * GROUP * U : (g_a + n) * GROUP * U])
+
+        load_w1(k1_sb, k1)
+        load_w1(m1_sb, m1)
+        load_h0(0)
+        load_h0(1)
+        load_h0(2)
+        load_w2(k2_sb, k2)
+        load_w2(m2_sb, m2)
+        for c in range(3, len(CHUNKS)):
+            load_h0(c)
+
+        def spread_bias():
+            bias_ps = s2pool.tile([P, U], F32, name="bias_ps", tag="s2")
+            nc.tensor.matmul(out=bias_ps[:], lhsT=ones[:], rhs=brow[:, 0:U], start=True, stop=True)
+            nc.vector.tensor_copy(out=bias_f[:], in_=bias_ps[:])
+            gain_ps = s2pool.tile([P, U], F32, name="gain_ps", tag="s2")
+            nc.tensor.matmul(out=gain_ps[:, 0:64], lhsT=ones[:], rhs=brow[:, U : U + 64], start=True, stop=True)
+            nc.vector.tensor_copy(out=gain_f[:], in_=gain_ps[:, 0:1])
+
+        bias_f = const.tile([P, U], F32, name="bias_f")
+        gain_f = const.tile([P, 1], F32, name="gain_f")
+
+        def quantise(src, name, pool):
+            codes = pool.tile([P, GCOLS], U32, name=name + "_c", tag=name + "_c", align_bytes=64)
+            scales = pool.tile([P, GCOLS], U8, name=name + "_s", tag=name + "_s", align_bytes=64)
+            nc.vector.quantize_mx(out=codes[:].bitcast(FP8X4), scales=scales[:], in_=src[:])
+            return codes, scales
+
+        def prepare_w1():
+            prod = const.tile([P, 4 * U], BF16, name="w1p")
+            nc.vector.tensor_tensor(out=prod[:], in0=k1_sb[:], in1=m1_sb[:], op=ALU.mult)
+            grouped = const.tile([P, 4 * U], BF16, name="w1g", align_bytes=64)
+            nc.vector.tensor_copy(
+                out=grouped[:].rearrange("p (s q t) -> p s q t", s=4, t=4),
+                in_=prod[:].rearrange("p (t q s) -> p s q t", t=4, s=4),
+            )
+            return quantise(grouped, "w1", const)
+
+        def prepare_w2():
+            prod = const.tile([P, 4 * U], BF16, name="w2p")
+            nc.vector.tensor_tensor(out=prod[:], in0=k2_sb[:], in1=m2_sb[:], op=ALU.mult)
+            grouped = const.tile([P, 4 * U], BF16, name="w2g", align_bytes=64)
+            nc.vector.tensor_copy(
+                out=grouped[:].rearrange("p (n j) -> p n j", j=4),
+                in_=prod[:].rearrange("p (j n) -> p n j", j=4),
+            )
+            return quantise(grouped, "w2", const)
+
+        g0_of = {}
+        q0_of = {}
+        g1_of = {}
+        q1_of = {}
+        y_of = {}
+        pending = {"V": [], "S": [], "T": []}
+        stores = []
+        emitted = {}
+        head_relu = []
+
+        def copy_on(engine, dst, src):
+            if engine == "S":
+                nc.scalar.copy(out=dst, in_=src)
+            else:
+                nc.vector.tensor_copy(out=dst, in_=src)
+
+        def transposes(g):
+            if g < 0 or g >= NG:
+                return
+            src, i = group_src[g]
+            words = src[:].bitcast(F32)
+            g0 = stage.tile([P, 4 * GCOLS], BF16, name="g0", tag="g0", align_bytes=64)
+            g0w = g0[:].bitcast(F32).rearrange("p (j r u) -> p j r u", j=GROUP, u=2)
+            for h in range(2):
+                tp = tpool.tile([P, 2, 2, P], F32, name="tp", tag="tp")
+                for jj in range(2):
+                    for u in range(2):
+                        w0 = (i * GROUP + 2 * h + jj) * (U // 2)
+                        nc.tensor.transpose(tp[:, jj, u, :], words[:, w0 + u : w0 + U // 2 : 2], ident[:])
+                copy_on(b_engine(g, h), g0w[:, 2 * h : 2 * h + 2, :, :], tp[:].rearrange("p j u r -> p j r u"))
+            g0_of[g] = g0
+
+        def quantise_h0(g):
+            if g < 0 or g >= NG:
+                return
+            q0_of[g] = quantise(g0_of[g], "q0", quant)
+
+        def stage1(g, jj):
+            if g < 0 or g >= NG:
+                return
+            if jj == 0:
+                g1_of[g] = stage.tile([P, 4 * GCOLS], BF16, name="g1", tag="g1", align_bytes=64)
+            g1v = g1_of[g][:].rearrange("p (j r t) -> p j r t", j=GROUP, t=4)
+            codes, scales = q0_of[g]
+            s1 = s1pool.tile([P, 4, P], F32, name="s1", tag="s1")
+            cols = slice(jj * P, (jj + 1) * P)
+            for t in range(4):
+                wcols = slice(t * P, (t + 1) * P)
+                nc.tensor.matmul_mx(
+                    out=s1[:, t, :],
+                    lhsT=w1c[:, wcols].bitcast(FP8X4),
+                    lhsT_scale=w1s[:, wcols],
+                    rhs=codes[:, cols].bitcast(FP8X4),
+                    rhs_scale=scales[:, cols],
+                    start=True,
+                    stop=True,
+                )
+            copy_on(e_engine(g, jj), g1v[:, jj, :, :], s1[:].rearrange("p t r -> p r t"))
+
+        def quantise_h1(g):
+            if g < 0 or g >= NG:
+                return
+            parts = f_split(g)
+            codes = quant.tile([P, GCOLS], U32, name="q1_c", tag="q1_c", align_bytes=64)
+            scales = quant.tile([P, GCOLS], U8, name="q1_s", tag="q1_s", align_bytes=64)
+            w = GCOLS // parts
+            for i in range(parts):
+                nc.vector.quantize_mx(
+                    out=codes[:, i * w : (i + 1) * w].bitcast(FP8X4),
+                    scales=scales[:, i * w : (i + 1) * w],
+                    in_=g1_of[g][:, 4 * i * w : 4 * (i + 1) * w],
+                )
+            q1_of[g] = (codes, scales)
+
+        def slots(k):
+            return max(0, OFF - GROUP * k), min(GROUP, TILES - (GROUP * k - OFF))
+
+        def runs(k):
+            pat = pattern(k)
+            lo, hi = slots(k)
+            res = []
+            a = lo
+            while a < hi:
+                b = a + 1
+                while (not per_tile(k)) and b < hi and pat[b] == pat[a]:
+                    b += 1
+                res.append((pat[a], a, b))
+                a = b
+            return res
+
+        def relu(k, run):
+            engine, a, b = run
+            ap = y_of[k][:, a * U : b * U]
+            if engine == "T":
+                y = y_of[k]
+                nc.vector.memset(y[:, GROUP * U : GROUP * U + PAD], 0.0)
+                rest = y[:, S_COLS:]
+                nc.gpsimd.tensor_scalar(out=rest, in0=rest, scalar1=FLT_MAX, scalar2=0.0, op0=ALU.min, op1=ALU.max)
+            elif engine == "G":
+                nc.gpsimd.tensor_scalar(out=ap, in0=ap, scalar1=FLT_MAX, scalar2=0.0, op0=ALU.min, op1=ALU.max)
+            elif engine == "V":
+                nc.vector.tensor_scalar(out=ap, in0=ap, scalar1=0.0, scalar2=None, op0=ALU.max)
+            else:
+                nc.scalar.activation(out=ap, in_=ap, func=ACT.Relu)
+            emitted[k] = emitted.get(k, 0) + 1
+            if per_tile(k):
+                if b % STORE_TILES == 0:
+                    stores.append((k, b - STORE_TILES, b))
+            elif emitted[k] == len(runs(k)):
+                lo, hi = slots(k)
+                stores.append((k, lo, hi))
+
+        def stage2(g, jj):
+            if g < 0 or g >= NG:
+                return
+            tile_no = g * GROUP + jj
+            k = (tile_no + OFF) // GROUP
+            slot = (tile_no + OFF) % GROUP
+            if k not in y_of:
+                y_of[k] = ypool.tile([P, GROUP * U + PAD], F32, name="y", tag="y")
+            y = y_of[k]
+            codes, scales = q1_of[g]
+            cols = slice(jj * P, (jj + 1) * P)
+            s2 = s2pool.tile([P, U], F32, name="s2", tag="s2")
+            nc.tensor.matmul_mx(
+                out=s2[:],
+                lhsT=codes[:, cols].bitcast(FP8X4),
+                lhsT_scale=scales[:, cols],
+                rhs=w2c[:].bitcast(FP8X4),
+                rhs_scale=w2s[:],
+                start=True,
+                stop=True,
+            )
+            nc.vector.scalar_tensor_tensor(
+                out=y[:, slot * U : (slot + 1) * U],
+                in0=s2[:],
+                scalar=gain_f[:, 0:1],
+                in1=bias_f[:],
+                op0=ALU.mult,
+                op1=ALU.add,
+            )
+            if pattern(k) == "TTTT" and slot == 0 and S_COLS:
+                head_relu.append(k)
+            for run in runs(k):
+                if run[2] - 1 == slot:
+                    if run[0] == "G":
+                        relu(k, run)
+                    else:
+                        pending[run[0]].append((k, run))
+
+        def flush_head_relu():
+            for k in head_relu:
+                ap = y_of[k][:, 0:S_COLS]
+                nc.scalar.activation(out=ap, in_=ap, func=ACT.Relu)
+            head_relu[:] = []
+
+        def flush(engine):
+            for k, run in pending[engine]:
+                relu(k, run)
+            pending[engine] = []
+
+        def store():
+            for k, a, b in stores:
+                first = GROUP * k - OFF
+                nc.sync.dma_start(
+                    out=outv[:, first + a : first + b, :],
+                    in_=y_of[k][:, a * U : b * U].rearrange("p (j n) -> p j n", n=U),
+                )
+            stores[:] = []
+
+        w1c, w1s = prepare_w1()
+        for g in range(LAG_A):
+            transposes(g)
+        for g in range(LAG_C):
+            quantise_h0(g)
+        spread_bias()
+        w2c, w2s = prepare_w2()
+        for s in range(NG + LAG_G):
+            for jj in range(GROUP):
+                stage1(s, jj)
+                stage2(s - LAG_G, jj)
+            flush("V")
+            transposes(s + LAG_A)
+            flush("S")
+            flush_head_relu()
+            store()
+            quantise_h1(s)
+            quantise_h0(s + LAG_C)
+            flush("T")
+            store()

@@ -20,38 +20,22 @@ NG = TILES // GROUP
 GCOLS = GROUP * P
 FLT_MAX = 3.4028234663852886e38
 PAD = 8
-STORE_TILES = 2
-S_COLS = 256
 FLOPS = 2 * 2 * ROWS * U * U
 
-CHUNKS = [1, 1, 2, 4, 4, 4]
+L2 = 6
 LAG_A = 3
 LAG_C = 2
-LAG_G = 2
-MANUAL = True
-OFF = 0
-NK = NG + (1 if OFF else 0)
-Y_BUFS = 6
+HEAD_T = 2
+S_COLS = 256
+LOADS = ["w1", (0, 1), (1, 2), "w2", (2, 3), (3, 4), (4, 5), (5, 6), (6, 7), (7, 8), (8, 12), (12, 16)]
+W2_STEP = 0
+RS_LAG = 4
+STORE_TILES = 1
+NSTEPS = NG + (L2 + GROUP - 1) // GROUP
 
 
-def pattern(k):
-    return "SSSS" if k >= 12 else "TTTT"
-
-
-def per_tile(k):
-    return k >= 12
-
-
-def e_engine(g, jj):
-    return "S"
-
-
-def b_engine(g, h):
-    return "S"
-
-
-def f_split(g):
-    return 1
+def relu_plan(st):
+    return "STST" if st >= NG else ("SSSS" if st >= NG - 1 else ("SGGG" if st >= NG - LAG_A else "GGGG"))
 
 
 def tile_sparsefactorisationdense_pa_t_kernel(tc, h0, k1, k2, m1, m2, scaling, bias, out):
@@ -60,12 +44,11 @@ def tile_sparsefactorisationdense_pa_t_kernel(tc, h0, k1, k2, m1, m2, scaling, b
         const = ctx.enter_context(tc.tile_pool(name="const", bufs=1))
         stage = ctx.enter_context(tc.tile_pool(name="stage", bufs=4))
         quant = ctx.enter_context(tc.tile_pool(name="quant", bufs=5))
-        ypool = ctx.enter_context(tc.tile_pool(name="ypool", bufs=Y_BUFS))
+        ypool = ctx.enter_context(tc.tile_pool(name="ypool", bufs=6))
         tpool = ctx.enter_context(tc.psum_pool(name="tpool", bufs=2))
         s1pool = ctx.enter_context(tc.psum_pool(name="s1pool", bufs=3))
         s2pool = ctx.enter_context(tc.psum_pool(name="s2pool", bufs=3))
-        if MANUAL:
-            ctx.enter_context(tc.manual_schedule())
+        ctx.enter_context(tc.manual_schedule())
 
         h0v = h0.rearrange("(p j) k -> p (j k)", j=TILES)
         outv = out.rearrange("(p j) n -> p j n", j=TILES)
@@ -82,40 +65,23 @@ def tile_sparsefactorisationdense_pa_t_kernel(tc, h0, k1, k2, m1, m2, scaling, b
         ident = const.tile([P, P], F32, name="ident")
         masks.make_identity(nc, ident[:])
 
-        k1_sb = const.tile([P, 4 * U], BF16, name="k1_sb")
-        m1_sb = const.tile([P, 4 * U], BF16, name="m1_sb")
-        k2_sb = const.tile([P, 4 * U], BF16, name="k2_sb")
-        m2_sb = const.tile([P, 4 * U], BF16, name="m2_sb")
+        w_sb = {}
+        group_src = {}
+        for item in LOADS:
+            if item in ("w1", "w2"):
+                for name, src in (("k", k1 if item == "w1" else k2), ("m", m1 if item == "w1" else m2)):
+                    t = const.tile([P, 4 * U], BF16, name=name + item)
+                    nc.sync.dma_start(out=t[:], in_=src.rearrange("(p j) c -> p (j c)", j=4))
+                    w_sb[name + item] = t
+            else:
+                g_a, g_b = item
+                t = const.tile([P, (g_b - g_a) * GROUP * U], BF16, name="h0g%d" % g_a)
+                nc.sync.dma_start(out=t[:], in_=h0v[:, g_a * GROUP * U : g_b * GROUP * U])
+                for g in range(g_a, g_b):
+                    group_src[g] = (t, g - g_a)
 
-        def load_w1(dst, src):
-            nc.sync.dma_start(out=dst[:], in_=src.rearrange("(p j) c -> p (j c)", j=4))
-
-        def load_w2(dst, src):
-            nc.sync.dma_start(out=dst[:], in_=src.rearrange("(p j) c -> p (j c)", j=4))
-
-        h0_tiles = []
-        group_src = []
-        g_first = 0
-        for c, n in enumerate(CHUNKS):
-            t = const.tile([P, n * GROUP * U], BF16, name="h0c%d" % c)
-            h0_tiles.append((t, g_first, n))
-            for i in range(n):
-                group_src.append((t, i))
-            g_first += n
-
-        def load_h0(c):
-            t, g_a, n = h0_tiles[c]
-            nc.sync.dma_start(out=t[:], in_=h0v[:, g_a * GROUP * U : (g_a + n) * GROUP * U])
-
-        load_w1(k1_sb, k1)
-        load_w1(m1_sb, m1)
-        load_h0(0)
-        load_h0(1)
-        load_h0(2)
-        load_w2(k2_sb, k2)
-        load_w2(m2_sb, m2)
-        for c in range(3, len(CHUNKS)):
-            load_h0(c)
+        bias_f = const.tile([P, U], F32, name="bias_f")
+        gain_f = const.tile([P, 1], F32, name="gain_f")
 
         def spread_bias():
             bias_ps = s2pool.tile([P, U], F32, name="bias_ps", tag="s2")
@@ -125,54 +91,36 @@ def tile_sparsefactorisationdense_pa_t_kernel(tc, h0, k1, k2, m1, m2, scaling, b
             nc.tensor.matmul(out=gain_ps[:, 0:64], lhsT=ones[:], rhs=brow[:, U : U + 64], start=True, stop=True)
             nc.vector.tensor_copy(out=gain_f[:], in_=gain_ps[:, 0:1])
 
-        bias_f = const.tile([P, U], F32, name="bias_f")
-        gain_f = const.tile([P, 1], F32, name="gain_f")
-
         def quantise(src, name, pool):
             codes = pool.tile([P, GCOLS], U32, name=name + "_c", tag=name + "_c", align_bytes=64)
             scales = pool.tile([P, GCOLS], U8, name=name + "_s", tag=name + "_s", align_bytes=64)
             nc.vector.quantize_mx(out=codes[:].bitcast(FP8X4), scales=scales[:], in_=src[:])
             return codes, scales
 
-        def prepare_w1():
-            prod = const.tile([P, 4 * U], BF16, name="w1p")
-            nc.vector.tensor_tensor(out=prod[:], in0=k1_sb[:], in1=m1_sb[:], op=ALU.mult)
-            grouped = const.tile([P, 4 * U], BF16, name="w1g", align_bytes=64)
-            nc.vector.tensor_copy(
-                out=grouped[:].rearrange("p (s q t) -> p s q t", s=4, t=4),
-                in_=prod[:].rearrange("p (t q s) -> p s q t", t=4, s=4),
-            )
-            return quantise(grouped, "w1", const)
-
-        def prepare_w2():
-            prod = const.tile([P, 4 * U], BF16, name="w2p")
-            nc.vector.tensor_tensor(out=prod[:], in0=k2_sb[:], in1=m2_sb[:], op=ALU.mult)
-            grouped = const.tile([P, 4 * U], BF16, name="w2g", align_bytes=64)
-            nc.vector.tensor_copy(
-                out=grouped[:].rearrange("p (n j) -> p n j", j=4),
-                in_=prod[:].rearrange("p (j n) -> p n j", j=4),
-            )
-            return quantise(grouped, "w2", const)
+        def prepare_w(item):
+            prod = const.tile([P, 4 * U], BF16, name=item + "p")
+            nc.vector.tensor_tensor(out=prod[:], in0=w_sb["k" + item][:], in1=w_sb["m" + item][:], op=ALU.mult)
+            grouped = const.tile([P, 4 * U], BF16, name=item + "g", align_bytes=64)
+            if item == "w1":
+                nc.vector.tensor_copy(
+                    out=grouped[:].rearrange("p (s q t) -> p s q t", s=4, t=4),
+                    in_=prod[:].rearrange("p (t q s) -> p s q t", t=4, s=4),
+                )
+            else:
+                nc.vector.tensor_copy(
+                    out=grouped[:].rearrange("p (n j) -> p n j", j=4),
+                    in_=prod[:].rearrange("p (j n) -> p n j", j=4),
+                )
+            return quantise(grouped, item, const)
 
         g0_of = {}
         q0_of = {}
         g1_of = {}
         q1_of = {}
         y_of = {}
-        pending = {"V": [], "S": [], "T": []}
-        stores = []
-        emitted = {}
-        head_relu = []
-
-        def copy_on(engine, dst, src):
-            if engine == "S":
-                nc.scalar.copy(out=dst, in_=src)
-            else:
-                nc.vector.tensor_copy(out=dst, in_=src)
+        w_q = {}
 
         def transposes(g):
-            if g < 0 or g >= NG:
-                return
             src, i = group_src[g]
             words = src[:].bitcast(F32)
             g0 = stage.tile([P, 4 * GCOLS], BF16, name="g0", tag="g0", align_bytes=64)
@@ -183,21 +131,18 @@ def tile_sparsefactorisationdense_pa_t_kernel(tc, h0, k1, k2, m1, m2, scaling, b
                     for u in range(2):
                         w0 = (i * GROUP + 2 * h + jj) * (U // 2)
                         nc.tensor.transpose(tp[:, jj, u, :], words[:, w0 + u : w0 + U // 2 : 2], ident[:])
-                copy_on(b_engine(g, h), g0w[:, 2 * h : 2 * h + 2, :, :], tp[:].rearrange("p j u r -> p j r u"))
+                nc.scalar.copy(out=g0w[:, 2 * h : 2 * h + 2, :, :], in_=tp[:].rearrange("p j u r -> p j r u"))
             g0_of[g] = g0
 
         def quantise_h0(g):
-            if g < 0 or g >= NG:
-                return
             q0_of[g] = quantise(g0_of[g], "q0", quant)
 
         def stage1(g, jj):
-            if g < 0 or g >= NG:
-                return
             if jj == 0:
                 g1_of[g] = stage.tile([P, 4 * GCOLS], BF16, name="g1", tag="g1", align_bytes=64)
             g1v = g1_of[g][:].rearrange("p (j r t) -> p j r t", j=GROUP, t=4)
             codes, scales = q0_of[g]
+            w1c, w1s = w_q["w1"]
             s1 = s1pool.tile([P, 4, P], F32, name="s1", tag="s1")
             cols = slice(jj * P, (jj + 1) * P)
             for t in range(4):
@@ -211,71 +156,15 @@ def tile_sparsefactorisationdense_pa_t_kernel(tc, h0, k1, k2, m1, m2, scaling, b
                     start=True,
                     stop=True,
                 )
-            copy_on(e_engine(g, jj), g1v[:, jj, :, :], s1[:].rearrange("p t r -> p r t"))
+            nc.scalar.copy(out=g1v[:, jj, :, :], in_=s1[:].rearrange("p t r -> p r t"))
 
         def quantise_h1(g):
-            if g < 0 or g >= NG:
-                return
-            parts = f_split(g)
-            codes = quant.tile([P, GCOLS], U32, name="q1_c", tag="q1_c", align_bytes=64)
-            scales = quant.tile([P, GCOLS], U8, name="q1_s", tag="q1_s", align_bytes=64)
-            w = GCOLS // parts
-            for i in range(parts):
-                nc.vector.quantize_mx(
-                    out=codes[:, i * w : (i + 1) * w].bitcast(FP8X4),
-                    scales=scales[:, i * w : (i + 1) * w],
-                    in_=g1_of[g][:, 4 * i * w : 4 * (i + 1) * w],
-                )
-            q1_of[g] = (codes, scales)
+            q1_of[g] = quantise(g1_of[g], "q1", quant)
 
-        def slots(k):
-            return max(0, OFF - GROUP * k), min(GROUP, TILES - (GROUP * k - OFF))
-
-        def runs(k):
-            pat = pattern(k)
-            lo, hi = slots(k)
-            res = []
-            a = lo
-            while a < hi:
-                b = a + 1
-                while (not per_tile(k)) and b < hi and pat[b] == pat[a]:
-                    b += 1
-                res.append((pat[a], a, b))
-                a = b
-            return res
-
-        def relu(k, run):
-            engine, a, b = run
-            ap = y_of[k][:, a * U : b * U]
-            if engine == "T":
-                y = y_of[k]
-                nc.vector.memset(y[:, GROUP * U : GROUP * U + PAD], 0.0)
-                rest = y[:, S_COLS:]
-                nc.gpsimd.tensor_scalar(out=rest, in0=rest, scalar1=FLT_MAX, scalar2=0.0, op0=ALU.min, op1=ALU.max)
-            elif engine == "G":
-                nc.gpsimd.tensor_scalar(out=ap, in0=ap, scalar1=FLT_MAX, scalar2=0.0, op0=ALU.min, op1=ALU.max)
-            elif engine == "V":
-                nc.vector.tensor_scalar(out=ap, in0=ap, scalar1=0.0, scalar2=None, op0=ALU.max)
-            else:
-                nc.scalar.activation(out=ap, in_=ap, func=ACT.Relu)
-            emitted[k] = emitted.get(k, 0) + 1
-            if per_tile(k):
-                if b % STORE_TILES == 0:
-                    stores.append((k, b - STORE_TILES, b))
-            elif emitted[k] == len(runs(k)):
-                lo, hi = slots(k)
-                stores.append((k, lo, hi))
-
-        def stage2(g, jj):
-            if g < 0 or g >= NG:
-                return
-            tile_no = g * GROUP + jj
-            k = (tile_no + OFF) // GROUP
-            slot = (tile_no + OFF) % GROUP
-            if k not in y_of:
-                y_of[k] = ypool.tile([P, GROUP * U + PAD], F32, name="y", tag="y")
-            y = y_of[k]
-            codes, scales = q1_of[g]
+        def stage2(tile_no, y, slot):
+            codes, scales = q1_of[tile_no // GROUP]
+            w2c, w2s = w_q["w2"]
+            jj = tile_no % GROUP
             cols = slice(jj * P, (jj + 1) * P)
             s2 = s2pool.tile([P, U], F32, name="s2", tag="s2")
             nc.tensor.matmul_mx(
@@ -295,52 +184,74 @@ def tile_sparsefactorisationdense_pa_t_kernel(tc, h0, k1, k2, m1, m2, scaling, b
                 op0=ALU.mult,
                 op1=ALU.add,
             )
-            if pattern(k) == "TTTT" and slot == 0 and S_COLS:
-                head_relu.append(k)
-            for run in runs(k):
-                if run[2] - 1 == slot:
-                    if run[0] == "G":
-                        relu(k, run)
-                    else:
-                        pending[run[0]].append((k, run))
 
-        def flush_head_relu():
-            for k in head_relu:
-                ap = y_of[k][:, 0:S_COLS]
-                nc.scalar.activation(out=ap, in_=ap, func=ACT.Relu)
-            head_relu[:] = []
+        def relu_scalar(y, a, b):
+            nc.scalar.activation(out=y[:, a:b], in_=y[:, a:b], func=ACT.Relu)
 
-        def flush(engine):
-            for k, run in pending[engine]:
-                relu(k, run)
-            pending[engine] = []
+        def store(y, first_tile, slot_a, slot_b):
+            nc.sync.dma_start(
+                out=outv[:, first_tile + slot_a : first_tile + slot_b, :],
+                in_=y[:, slot_a * U : slot_b * U].rearrange("p (j n) -> p j n", n=U),
+            )
 
-        def store():
-            for k, a, b in stores:
-                first = GROUP * k - OFF
-                nc.sync.dma_start(
-                    out=outv[:, first + a : first + b, :],
-                    in_=y_of[k][:, a * U : b * U].rearrange("p (j n) -> p j n", n=U),
-                )
-            stores[:] = []
-
-        w1c, w1s = prepare_w1()
-        for g in range(LAG_A):
+        w_q["w1"] = prepare_w("w1")
+        for g in range(HEAD_T):
             transposes(g)
-        for g in range(LAG_C):
             quantise_h0(g)
         spread_bias()
-        w2c, w2s = prepare_w2()
-        for s in range(NG + LAG_G):
+        next_t = HEAD_T
+        next_c = HEAD_T
+        for st in range(NSTEPS):
+            first = GROUP * st - L2
+            slots = [jj for jj in range(GROUP) if 0 <= first + jj < TILES]
+            plan = relu_plan(st) if len(slots) == GROUP else "SSSS"
+            g_slots = [jj for jj in slots if plan[jj] == "G"]
+            t_slots = [jj for jj in slots if plan[jj] != "G"]
+            y = None
+            if slots:
+                y = ypool.tile([P, GROUP * U + PAD], F32, name="y", tag="y")
+            waiting = []
+            unsaved = []
+
+            def tile_relus(upto):
+                for s in [w for w in waiting if w <= upto]:
+                    waiting.remove(s)
+                    if plan[s] == "S":
+                        relu_scalar(y, s * U, (s + 1) * U)
+                    else:
+                        ap = y[:, s * U : (s + 1) * U]
+                        nc.gpsimd.tensor_scalar(out=ap, in0=ap, scalar1=FLT_MAX, scalar2=0.0, op0=ALU.min, op1=ALU.max)
+                    unsaved.append(s)
+                    if len(unsaved) == STORE_TILES or s == t_slots[-1]:
+                        store(y, first, unsaved[0], unsaved[-1] + 1)
+                        unsaved.clear()
+
             for jj in range(GROUP):
-                stage1(s, jj)
-                stage2(s - LAG_G, jj)
-            flush("V")
-            transposes(s + LAG_A)
-            flush("S")
-            flush_head_relu()
-            store()
-            quantise_h1(s)
-            quantise_h0(s + LAG_C)
-            flush("T")
-            store()
+                if st < NG:
+                    stage1(st, jj)
+                    tile_relus(jj - RS_LAG)
+                if jj in slots:
+                    stage2(first + jj, y, jj)
+                    if jj in t_slots:
+                        waiting.append(jj)
+                    if st >= NG:
+                        tile_relus(jj)
+            while next_t < NG and next_t <= st + LAG_A:
+                transposes(next_t)
+                next_t += 1
+            tile_relus(GROUP)
+            if st == W2_STEP:
+                w_q["w2"] = prepare_w("w2")
+            if g_slots and not t_slots and S_COLS:
+                relu_scalar(y, 0, S_COLS)
+            if st < NG:
+                quantise_h1(st)
+            while next_c < NG and next_c <= st + LAG_C:
+                quantise_h0(next_c)
+                next_c += 1
+            if g_slots:
+                nc.vector.memset(y[:, GROUP * U : GROUP * U + PAD], 0.0)
+                lo = g_slots[0] * U + (0 if t_slots else S_COLS)
+                rest = y[:, lo:]
+                nc.gpsimd.tensor_scalar(out=rest, in0=rest, scalar1=FLT_MAX, scalar2=0.0, op0=ALU.min, op1=ALU.max)
+                store(y, first, g_slots[0], GROUP)

@@ -19,7 +19,6 @@ GROUP = 4
 NG = TILES // GROUP
 GCOLS = GROUP * P
 FLT_MAX = 3.4028234663852886e38
-PAD = 8
 FLOPS = 2 * 2 * ROWS * U * U
 
 L2 = 6
@@ -29,9 +28,16 @@ HEAD_T = 2
 S_COLS = 256
 LOADS = ["w1", (0, 1), (1, 2), "w2", (2, 3), (3, 4), (4, 5), (5, 6), (6, 7), (7, 8), (8, 12), (12, 16)]
 W2_STEP = 0
+V_COLS = 256
+LAP = 8
+STEP_ORDER = "a0 b0 a1 b1 a2 b2 a3 b3"
 RS_LAG = 4
 STORE_TILES = 1
 NSTEPS = NG + (L2 + GROUP - 1) // GROUP
+
+
+def t_limit(st):
+    return st + LAG_A
 
 
 def relu_plan(st):
@@ -66,7 +72,7 @@ def tile_sparsefactorisationdense_pa_t_kernel(tc, h0, k1, k2, m1, m2, scaling, b
         masks.make_identity(nc, ident[:])
 
         w_sb = {}
-        group_src = {}
+        tile_src = {}
         for item in LOADS:
             if item in ("w1", "w2"):
                 for name, src in (("k", k1 if item == "w1" else k2), ("m", m1 if item == "w1" else m2)):
@@ -74,11 +80,11 @@ def tile_sparsefactorisationdense_pa_t_kernel(tc, h0, k1, k2, m1, m2, scaling, b
                     nc.sync.dma_start(out=t[:], in_=src.rearrange("(p j) c -> p (j c)", j=4))
                     w_sb[name + item] = t
             else:
-                g_a, g_b = item
-                t = const.tile([P, (g_b - g_a) * GROUP * U], BF16, name="h0g%d" % g_a)
-                nc.sync.dma_start(out=t[:], in_=h0v[:, g_a * GROUP * U : g_b * GROUP * U])
-                for g in range(g_a, g_b):
-                    group_src[g] = (t, g - g_a)
+                t_a, t_b = 4 * item[0], 4 * item[1]
+                t = const.tile([P, (t_b - t_a) * U], BF16, name="h0t%d" % t_a)
+                nc.sync.dma_start(out=t[:], in_=h0v[:, t_a * U : t_b * U])
+                for i in range(t_a, t_b):
+                    tile_src[i] = (t, i - t_a)
 
         bias_f = const.tile([P, U], F32, name="bias_f")
         gain_f = const.tile([P, 1], F32, name="gain_f")
@@ -91,14 +97,14 @@ def tile_sparsefactorisationdense_pa_t_kernel(tc, h0, k1, k2, m1, m2, scaling, b
             nc.tensor.matmul(out=gain_ps[:, 0:64], lhsT=ones[:], rhs=brow[:, U : U + 64], start=True, stop=True)
             nc.vector.tensor_copy(out=gain_f[:], in_=gain_ps[:, 0:1])
 
-        def quantise(src, name, pool):
-            codes = pool.tile([P, GCOLS], U32, name=name + "_c", tag=name + "_c", align_bytes=64)
-            scales = pool.tile([P, GCOLS], U8, name=name + "_s", tag=name + "_s", align_bytes=64)
+        def quantise(src, name, pool, width=GCOLS):
+            codes = pool.tile([P, width], U32, name=name + "_c", tag=name + "_c", align_bytes=64)
+            scales = pool.tile([P, width], U8, name=name + "_s", tag=name + "_s", align_bytes=64)
             nc.vector.quantize_mx(out=codes[:].bitcast(FP8X4), scales=scales[:], in_=src[:])
             return codes, scales
 
         def prepare_w(item):
-            prod = const.tile([P, 4 * U], BF16, name=item + "p")
+            prod = w_sb["k" + item]
             nc.vector.tensor_tensor(out=prod[:], in0=w_sb["k" + item][:], in1=w_sb["m" + item][:], op=ALU.mult)
             grouped = const.tile([P, 4 * U], BF16, name=item + "g", align_bytes=64)
             if item == "w1":
@@ -111,7 +117,7 @@ def tile_sparsefactorisationdense_pa_t_kernel(tc, h0, k1, k2, m1, m2, scaling, b
                     out=grouped[:].rearrange("p (n j) -> p n j", j=4),
                     in_=prod[:].rearrange("p (j n) -> p n j", j=4),
                 )
-            return quantise(grouped, item, const)
+            return quantise(grouped, item, const, U)
 
         g0_of = {}
         q0_of = {}
@@ -121,15 +127,15 @@ def tile_sparsefactorisationdense_pa_t_kernel(tc, h0, k1, k2, m1, m2, scaling, b
         w_q = {}
 
         def transposes(g):
-            src, i = group_src[g]
-            words = src[:].bitcast(F32)
             g0 = stage.tile([P, 4 * GCOLS], BF16, name="g0", tag="g0", align_bytes=64)
             g0w = g0[:].bitcast(F32).rearrange("p (j r u) -> p j r u", j=GROUP, u=2)
-            for h in range(2):
+            for h in range(GROUP // 2):
                 tp = tpool.tile([P, 2, 2, P], F32, name="tp", tag="tp")
                 for jj in range(2):
+                    src, i = tile_src[g * GROUP + 2 * h + jj]
+                    words = src[:].bitcast(F32)
                     for u in range(2):
-                        w0 = (i * GROUP + 2 * h + jj) * (U // 2)
+                        w0 = i * (U // 2)
                         nc.tensor.transpose(tp[:, jj, u, :], words[:, w0 + u : w0 + U // 2 : 2], ident[:])
                 nc.scalar.copy(out=g0w[:, 2 * h : 2 * h + 2, :, :], in_=tp[:].rearrange("p j u r -> p j r u"))
             g0_of[g] = g0
@@ -204,12 +210,12 @@ def tile_sparsefactorisationdense_pa_t_kernel(tc, h0, k1, k2, m1, m2, scaling, b
         for st in range(NSTEPS):
             first = GROUP * st - L2
             slots = [jj for jj in range(GROUP) if 0 <= first + jj < TILES]
-            plan = relu_plan(st) if len(slots) == GROUP else "SSSS"
+            plan = relu_plan(st) if len(slots) == GROUP else "S" * GROUP
             g_slots = [jj for jj in slots if plan[jj] == "G"]
             t_slots = [jj for jj in slots if plan[jj] != "G"]
             y = None
             if slots:
-                y = ypool.tile([P, GROUP * U + PAD], F32, name="y", tag="y")
+                y = ypool.tile([P, GROUP * U], F32, name="y", tag="y")
             waiting = []
             unsaved = []
 
@@ -226,17 +232,18 @@ def tile_sparsefactorisationdense_pa_t_kernel(tc, h0, k1, k2, m1, m2, scaling, b
                         store(y, first, unsaved[0], unsaved[-1] + 1)
                         unsaved.clear()
 
-            for jj in range(GROUP):
-                if st < NG:
+            for word in STEP_ORDER.split():
+                jj = int(word[1])
+                if word[0] == "a" and st < NG:
                     stage1(st, jj)
                     tile_relus(jj - RS_LAG)
-                if jj in slots:
+                if word[0] == "b" and jj in slots:
                     stage2(first + jj, y, jj)
                     if jj in t_slots:
                         waiting.append(jj)
                     if st >= NG:
                         tile_relus(jj)
-            while next_t < NG and next_t <= st + LAG_A:
+            while next_t < NG and next_t <= t_limit(st):
                 transposes(next_t)
                 next_t += 1
             tile_relus(GROUP)
@@ -250,8 +257,9 @@ def tile_sparsefactorisationdense_pa_t_kernel(tc, h0, k1, k2, m1, m2, scaling, b
                 quantise_h0(next_c)
                 next_c += 1
             if g_slots:
-                nc.vector.memset(y[:, GROUP * U : GROUP * U + PAD], 0.0)
                 lo = g_slots[0] * U + (0 if t_slots else S_COLS)
-                rest = y[:, lo:]
+                mine = y[:, lo : lo + V_COLS]
+                nc.vector.tensor_scalar(out=mine, in0=mine, scalar1=0.0, scalar2=None, op0=ALU.max)
+                rest = y[:, lo + V_COLS - LAP : GROUP * U]
                 nc.gpsimd.tensor_scalar(out=rest, in0=rest, scalar1=FLT_MAX, scalar2=0.0, op0=ALU.min, op1=ALU.max)
                 store(y, first, g_slots[0], GROUP)

@@ -25,7 +25,7 @@ L2 = 6
 LAG_A = 3
 LAG_C = 2
 HEAD_T = 2
-S_COLS = 256
+S_COLS = 0
 LOADS = ["w1", (0, 1), (1, 2), "w2", (2, 3), (3, 4), (4, 5), (5, 6), (6, 7), (7, 8), (8, 12), (12, 16)]
 W2_STEP = 0
 V_COLS = 256

@@ -28,16 +28,23 @@ HEAD_T = 2
 S_COLS = 0
 LOADS = ["w1", (0, 1), (1, 2), "w2", (2, 3), (3, 4), (4, 5), (5, 6), (6, 7), (7, 8), (8, 12), (12, 16)]
 W2_STEP = 0
+T_PAIRS = False
+HEAD_DEFER = ()
+BIAS_ON_S = False
+FUSED = False
+DEFER = "c0" in "a0 b0 a1 b1 a2 b2 a3 b3 t0 t1"
+V_ORDER = "F C"
+E_BLOCK = 0
 V_COLS = 256
 LAP = 8
-STEP_ORDER = "a0 b0 a1 b1 a2 b2 a3 b3"
+STEP_ORDER = "a0 b0 a1 b1 a2 b2 a3 b3 t0 t1"
 RS_LAG = 4
 STORE_TILES = 1
 NSTEPS = NG + (L2 + GROUP - 1) // GROUP
 
 
-def t_limit(st):
-    return st + LAG_A
+def vector_takes(g, h):
+    return g in (3, 4)
 
 
 def relu_plan(st):
@@ -51,9 +58,8 @@ def tile_sparsefactorisationdense_pa_t_kernel(tc, h0, k1, k2, m1, m2, scaling, b
         stage = ctx.enter_context(tc.tile_pool(name="stage", bufs=4))
         quant = ctx.enter_context(tc.tile_pool(name="quant", bufs=5))
         ypool = ctx.enter_context(tc.tile_pool(name="ypool", bufs=6))
-        tpool = ctx.enter_context(tc.psum_pool(name="tpool", bufs=2))
         s1pool = ctx.enter_context(tc.psum_pool(name="s1pool", bufs=3))
-        s2pool = ctx.enter_context(tc.psum_pool(name="s2pool", bufs=3))
+        xpool = ctx.enter_context(tc.psum_pool(name="xpool", bufs=5))
         ctx.enter_context(tc.manual_schedule())
 
         h0v = h0.rearrange("(p j) k -> p (j k)", j=TILES)
@@ -90,12 +96,18 @@ def tile_sparsefactorisationdense_pa_t_kernel(tc, h0, k1, k2, m1, m2, scaling, b
         gain_f = const.tile([P, 1], F32, name="gain_f")
 
         def spread_bias():
-            bias_ps = s2pool.tile([P, U], F32, name="bias_ps", tag="s2")
+            bias_ps = xpool.tile([P, U], F32, name="bias_ps", tag="x")
             nc.tensor.matmul(out=bias_ps[:], lhsT=ones[:], rhs=brow[:, 0:U], start=True, stop=True)
-            nc.vector.tensor_copy(out=bias_f[:], in_=bias_ps[:])
-            gain_ps = s2pool.tile([P, U], F32, name="gain_ps", tag="s2")
+            if BIAS_ON_S:
+                nc.scalar.copy(out=bias_f[:], in_=bias_ps[:])
+            else:
+                nc.vector.tensor_copy(out=bias_f[:], in_=bias_ps[:])
+            gain_ps = xpool.tile([P, U], F32, name="gain_ps", tag="x")
             nc.tensor.matmul(out=gain_ps[:, 0:64], lhsT=ones[:], rhs=brow[:, U : U + 64], start=True, stop=True)
-            nc.vector.tensor_copy(out=gain_f[:], in_=gain_ps[:, 0:1])
+            if BIAS_ON_S:
+                nc.scalar.copy(out=gain_f[:], in_=gain_ps[:, 0:1])
+            else:
+                nc.vector.tensor_copy(out=gain_f[:], in_=gain_ps[:, 0:1])
 
         def quantise(src, name, pool, width=GCOLS):
             codes = pool.tile([P, width], U32, name=name + "_c", tag=name + "_c", align_bytes=64)
@@ -104,21 +116,25 @@ def tile_sparsefactorisationdense_pa_t_kernel(tc, h0, k1, k2, m1, m2, scaling, b
             return codes, scales
 
         def prepare_w(item):
-            prod = w_sb["k" + item]
-            nc.vector.tensor_tensor(out=prod[:], in0=w_sb["k" + item][:], in1=w_sb["m" + item][:], op=ALU.mult)
+            kk, mm = w_sb["k" + item], w_sb["m" + item]
             grouped = const.tile([P, 4 * U], BF16, name=item + "g", align_bytes=64)
-            if item == "w1":
-                nc.vector.tensor_copy(
-                    out=grouped[:].rearrange("p (s q t) -> p s q t", s=4, t=4),
-                    in_=prod[:].rearrange("p (t q s) -> p s q t", t=4, s=4),
+            dst_view = "p (s q t) -> p s q t" if item == "w1" else "p (s q t) -> p q s t"
+            dst = grouped[:].rearrange(dst_view, s=4 if item == "w1" else 1, t=4)
+            src_view = "p (t q s) -> p s q t" if item == "w1" else "p (t q s) -> p q s t"
+            if FUSED:
+                nc.vector.tensor_tensor(
+                    out=dst,
+                    in0=kk[:].rearrange(src_view, t=4, s=4 if item == "w1" else 1),
+                    in1=mm[:].rearrange(src_view, t=4, s=4 if item == "w1" else 1),
+                    op=ALU.mult,
                 )
             else:
-                nc.vector.tensor_copy(
-                    out=grouped[:].rearrange("p (n j) -> p n j", j=4),
-                    in_=prod[:].rearrange("p (j n) -> p n j", j=4),
-                )
+                nc.vector.tensor_tensor(out=kk[:], in0=kk[:], in1=mm[:], op=ALU.mult)
+                nc.vector.tensor_copy(out=dst, in_=kk[:].rearrange(src_view, t=4, s=4 if item == "w1" else 1))
             return quantise(grouped, item, const, U)
 
+        late_copies = []
+        held = {}
         g0_of = {}
         q0_of = {}
         g1_of = {}
@@ -126,19 +142,29 @@ def tile_sparsefactorisationdense_pa_t_kernel(tc, h0, k1, k2, m1, m2, scaling, b
         y_of = {}
         w_q = {}
 
-        def transposes(g):
-            g0 = stage.tile([P, 4 * GCOLS], BF16, name="g0", tag="g0", align_bytes=64)
-            g0w = g0[:].bitcast(F32).rearrange("p (j r u) -> p j r u", j=GROUP, u=2)
+        def transpose_bank(g, h, defer=False):
+            if h == 0:
+                g0_of[g] = stage.tile([P, 4 * GCOLS], BF16, name="g0", tag="g0", align_bytes=64)
+            g0w = g0_of[g][:].bitcast(F32).rearrange("p (j r u) -> p j r u", j=GROUP, u=2)
+            tp = xpool.tile([P, 2, 2, P], F32, name="tp", tag="x")
+            for jj in range(2):
+                src, i = tile_src[g * GROUP + 2 * h + jj]
+                words = src[:].bitcast(F32)
+                for u in range(2):
+                    w0 = i * (U // 2)
+                    nc.tensor.transpose(tp[:, jj, u, :], words[:, w0 + u : w0 + U // 2 : 2], ident[:])
+            pair = (g0w[:, 2 * h : 2 * h + 2, :, :], tp[:].rearrange("p j u r -> p j r u"))
+            if vector_takes(g, h):
+                late_copies.append(pair)
+            elif defer:
+                assert held.get(h) is None
+                held[h] = pair
+            else:
+                nc.scalar.copy(out=pair[0], in_=pair[1])
+
+        def transposes(g, defer=False):
             for h in range(GROUP // 2):
-                tp = tpool.tile([P, 2, 2, P], F32, name="tp", tag="tp")
-                for jj in range(2):
-                    src, i = tile_src[g * GROUP + 2 * h + jj]
-                    words = src[:].bitcast(F32)
-                    for u in range(2):
-                        w0 = i * (U // 2)
-                        nc.tensor.transpose(tp[:, jj, u, :], words[:, w0 + u : w0 + U // 2 : 2], ident[:])
-                nc.scalar.copy(out=g0w[:, 2 * h : 2 * h + 2, :, :], in_=tp[:].rearrange("p j u r -> p j r u"))
-            g0_of[g] = g0
+                transpose_bank(g, h, defer)
 
         def quantise_h0(g):
             q0_of[g] = quantise(g0_of[g], "q0", quant)
@@ -146,7 +172,10 @@ def tile_sparsefactorisationdense_pa_t_kernel(tc, h0, k1, k2, m1, m2, scaling, b
         def stage1(g, jj):
             if jj == 0:
                 g1_of[g] = stage.tile([P, 4 * GCOLS], BF16, name="g1", tag="g1", align_bytes=64)
-            g1v = g1_of[g][:].rearrange("p (j r t) -> p j r t", j=GROUP, t=4)
+            if E_BLOCK:
+                g1v = g1_of[g][:].rearrange("p (j c i t) -> p j c t i", j=GROUP, i=E_BLOCK, t=4)
+            else:
+                g1v = g1_of[g][:].rearrange("p (j r t) -> p j r t", j=GROUP, t=4)
             codes, scales = q0_of[g]
             w1c, w1s = w_q["w1"]
             s1 = s1pool.tile([P, 4, P], F32, name="s1", tag="s1")
@@ -162,7 +191,10 @@ def tile_sparsefactorisationdense_pa_t_kernel(tc, h0, k1, k2, m1, m2, scaling, b
                     start=True,
                     stop=True,
                 )
-            nc.scalar.copy(out=g1v[:, jj, :, :], in_=s1[:].rearrange("p t r -> p r t"))
+            if E_BLOCK:
+                nc.scalar.copy(out=g1v[:, jj], in_=s1[:].rearrange("p t (c i) -> p c t i", i=E_BLOCK))
+            else:
+                nc.scalar.copy(out=g1v[:, jj, :, :], in_=s1[:].rearrange("p t r -> p r t"))
 
         def quantise_h1(g):
             q1_of[g] = quantise(g1_of[g], "q1", quant)
@@ -172,7 +204,7 @@ def tile_sparsefactorisationdense_pa_t_kernel(tc, h0, k1, k2, m1, m2, scaling, b
             w2c, w2s = w_q["w2"]
             jj = tile_no % GROUP
             cols = slice(jj * P, (jj + 1) * P)
-            s2 = s2pool.tile([P, U], F32, name="s2", tag="s2")
+            s2 = xpool.tile([P, U], F32, name="s2", tag="x")
             nc.tensor.matmul_mx(
                 out=s2[:],
                 lhsT=codes[:, cols].bitcast(FP8X4),
@@ -200,12 +232,14 @@ def tile_sparsefactorisationdense_pa_t_kernel(tc, h0, k1, k2, m1, m2, scaling, b
                 in_=y[:, slot_a * U : slot_b * U].rearrange("p (j n) -> p j n", n=U),
             )
 
+        if BIAS_ON_S:
+            spread_bias()
         w_q["w1"] = prepare_w("w1")
         for g in range(HEAD_T):
             transposes(g)
             quantise_h0(g)
-        spread_bias()
-        next_t = HEAD_T
+        if not BIAS_ON_S:
+            spread_bias()
         next_c = HEAD_T
         for st in range(NSTEPS):
             first = GROUP * st - L2
@@ -243,19 +277,30 @@ def tile_sparsefactorisationdense_pa_t_kernel(tc, h0, k1, k2, m1, m2, scaling, b
                         waiting.append(jj)
                     if st >= NG:
                         tile_relus(jj)
-            while next_t < NG and next_t <= t_limit(st):
-                transposes(next_t)
-                next_t += 1
+                if word[0] == "t" and 0 < st and st + LAG_A < NG:
+                    transpose_bank(st + LAG_A, jj, DEFER)
+                if word[0] == "c" and held.get(jj) is not None:
+                    nc.scalar.copy(out=held[jj][0], in_=held[jj][1])
+                    held[jj] = None
+            if st == 0:
+                for g in range(HEAD_T, LAG_A + 1):
+                    for h in range(GROUP // 2):
+                        transpose_bank(g, h, g == LAG_A and h in HEAD_DEFER)
+            elif T_PAIRS and st % 2 == 1:
+                for g in (st + LAG_A, st + LAG_A + 1):
+                    if g < NG:
+                        transposes(g)
             tile_relus(GROUP)
             if st == W2_STEP:
                 w_q["w2"] = prepare_w("w2")
             if g_slots and not t_slots and S_COLS:
                 relu_scalar(y, 0, S_COLS)
-            if st < NG:
-                quantise_h1(st)
-            while next_c < NG and next_c <= st + LAG_C:
-                quantise_h0(next_c)
-                next_c += 1
+            for word in V_ORDER.split():
+                if word == "F" and st < NG:
+                    quantise_h1(st)
+                while word == "C" and next_c < NG and next_c <= st + LAG_C:
+                    quantise_h0(next_c)
+                    next_c += 1
             if g_slots:
                 lo = g_slots[0] * U + (0 if t_slots else S_COLS)
                 mine = y[:, lo : lo + V_COLS]
@@ -263,3 +308,6 @@ def tile_sparsefactorisationdense_pa_t_kernel(tc, h0, k1, k2, m1, m2, scaling, b
                 rest = y[:, lo + V_COLS - LAP : GROUP * U]
                 nc.gpsimd.tensor_scalar(out=rest, in0=rest, scalar1=FLT_MAX, scalar2=0.0, op0=ALU.min, op1=ALU.max)
                 store(y, first, g_slots[0], GROUP)
+            for dst, src in late_copies:
+                nc.vector.tensor_copy(out=dst, in_=src)
+            late_copies.clear()

@@ -28,6 +28,10 @@ HEAD_T = 2
 S_COLS = 0
 LOADS = ["w1", (0, 1), (1, 2), "w2", (2, 3), (3, 4), (4, 5), (5, 6), (6, 7), (7, 8), (8, 12), (12, 16)]
 W2_STEP = 0
+S_INTERLEAVES = ()
+FIRST_PLAN = "SSSS"
+BIAS_LATE = True
+S_QUEUE = False
 T_PAIRS = False
 HEAD_DEFER = ()
 BIAS_ON_S = False
@@ -74,6 +78,8 @@ def tile_sparsefactorisationdense_pa_t_kernel(tc, h0, k1, k2, m1, m2, scaling, b
         nc.scalar.dma_start(out=brow[0:1, 0:U], in_=bias.rearrange("(o n) -> o n", o=1))
         nc.scalar.dma_start(out=brow[0:1, U : U + 1], in_=scaling.rearrange("(o n) -> o n", o=1))
         nc.scalar.activation(out=warm[:], in_=warm[:], func=ACT.Relu)
+        probe = const.tile([P, 8], U32, name="probe")
+        newest = [None]
         ident = const.tile([P, P], F32, name="ident")
         masks.make_identity(nc, ident[:])
 
@@ -95,16 +101,22 @@ def tile_sparsefactorisationdense_pa_t_kernel(tc, h0, k1, k2, m1, m2, scaling, b
         bias_f = const.tile([P, U], F32, name="bias_f")
         gain_f = const.tile([P, 1], F32, name="gain_f")
 
+        bias_copies = []
+
         def spread_bias():
             bias_ps = xpool.tile([P, U], F32, name="bias_ps", tag="x")
             nc.tensor.matmul(out=bias_ps[:], lhsT=ones[:], rhs=brow[:, 0:U], start=True, stop=True)
-            if BIAS_ON_S:
+            if BIAS_LATE:
+                bias_copies.append((bias_f[:], bias_ps[:]))
+            elif BIAS_ON_S:
                 nc.scalar.copy(out=bias_f[:], in_=bias_ps[:])
             else:
                 nc.vector.tensor_copy(out=bias_f[:], in_=bias_ps[:])
             gain_ps = xpool.tile([P, U], F32, name="gain_ps", tag="x")
             nc.tensor.matmul(out=gain_ps[:, 0:64], lhsT=ones[:], rhs=brow[:, U : U + 64], start=True, stop=True)
-            if BIAS_ON_S:
+            if BIAS_LATE:
+                bias_copies.append((gain_f[:], gain_ps[:, 0:1]))
+            elif BIAS_ON_S:
                 nc.scalar.copy(out=gain_f[:], in_=gain_ps[:, 0:1])
             else:
                 nc.vector.tensor_copy(out=gain_f[:], in_=gain_ps[:, 0:1])
@@ -113,6 +125,7 @@ def tile_sparsefactorisationdense_pa_t_kernel(tc, h0, k1, k2, m1, m2, scaling, b
             codes = pool.tile([P, width], U32, name=name + "_c", tag=name + "_c", align_bytes=64)
             scales = pool.tile([P, width], U8, name=name + "_s", tag=name + "_s", align_bytes=64)
             nc.vector.quantize_mx(out=codes[:].bitcast(FP8X4), scales=scales[:], in_=src[:])
+            newest[0] = codes
             return codes, scales
 
         def prepare_w(item):
@@ -130,7 +143,10 @@ def tile_sparsefactorisationdense_pa_t_kernel(tc, h0, k1, k2, m1, m2, scaling, b
                 )
             else:
                 nc.vector.tensor_tensor(out=kk[:], in0=kk[:], in1=mm[:], op=ALU.mult)
-                nc.vector.tensor_copy(out=dst, in_=kk[:].rearrange(src_view, t=4, s=4 if item == "w1" else 1))
+                if item in S_INTERLEAVES:
+                    nc.scalar.copy(out=dst, in_=kk[:].rearrange(src_view, t=4, s=4 if item == "w1" else 1))
+                else:
+                    nc.vector.tensor_copy(out=dst, in_=kk[:].rearrange(src_view, t=4, s=4 if item == "w1" else 1))
             return quantise(grouped, item, const, U)
 
         late_copies = []
@@ -226,8 +242,8 @@ def tile_sparsefactorisationdense_pa_t_kernel(tc, h0, k1, k2, m1, m2, scaling, b
         def relu_scalar(y, a, b):
             nc.scalar.activation(out=y[:, a:b], in_=y[:, a:b], func=ACT.Relu)
 
-        def store(y, first_tile, slot_a, slot_b):
-            nc.sync.dma_start(
+        def store(y, first_tile, slot_a, slot_b, queue=None):
+            (queue or nc.sync).dma_start(
                 out=outv[:, first_tile + slot_a : first_tile + slot_b, :],
                 in_=y[:, slot_a * U : slot_b * U].rearrange("p (j n) -> p j n", n=U),
             )
@@ -244,7 +260,7 @@ def tile_sparsefactorisationdense_pa_t_kernel(tc, h0, k1, k2, m1, m2, scaling, b
         for st in range(NSTEPS):
             first = GROUP * st - L2
             slots = [jj for jj in range(GROUP) if 0 <= first + jj < TILES]
-            plan = relu_plan(st) if len(slots) == GROUP else "S" * GROUP
+            plan = relu_plan(st) if len(slots) == GROUP else (FIRST_PLAN if st < NG else "S" * GROUP)
             g_slots = [jj for jj in slots if plan[jj] == "G"]
             t_slots = [jj for jj in slots if plan[jj] != "G"]
             y = None
@@ -263,7 +279,7 @@ def tile_sparsefactorisationdense_pa_t_kernel(tc, h0, k1, k2, m1, m2, scaling, b
                         nc.gpsimd.tensor_scalar(out=ap, in0=ap, scalar1=FLT_MAX, scalar2=0.0, op0=ALU.min, op1=ALU.max)
                     unsaved.append(s)
                     if len(unsaved) == STORE_TILES or s == t_slots[-1]:
-                        store(y, first, unsaved[0], unsaved[-1] + 1)
+                        store(y, first, unsaved[0], unsaved[-1] + 1, nc.scalar if S_QUEUE and plan[s] == "S" else None)
                         unsaved.clear()
 
             for word in STEP_ORDER.split():
@@ -286,6 +302,8 @@ def tile_sparsefactorisationdense_pa_t_kernel(tc, h0, k1, k2, m1, m2, scaling, b
                 for g in range(HEAD_T, LAG_A + 1):
                     for h in range(GROUP // 2):
                         transpose_bank(g, h, g == LAG_A and h in HEAD_DEFER)
+                for dst, src in bias_copies:
+                    nc.scalar.copy(out=dst, in_=src)
             elif T_PAIRS and st % 2 == 1:
                 for g in (st + LAG_A, st + LAG_A + 1):
                     if g < NG:
@@ -303,9 +321,13 @@ def tile_sparsefactorisationdense_pa_t_kernel(tc, h0, k1, k2, m1, m2, scaling, b
                     next_c += 1
             if g_slots:
                 lo = g_slots[0] * U + (0 if t_slots else S_COLS)
-                mine = y[:, lo : lo + V_COLS]
-                nc.vector.tensor_scalar(out=mine, in0=mine, scalar1=0.0, scalar2=None, op0=ALU.max)
-                rest = y[:, lo + V_COLS - LAP : GROUP * U]
+                if V_COLS:
+                    mine = y[:, lo : lo + V_COLS]
+                    nc.vector.tensor_scalar(out=mine, in0=mine, scalar1=0.0, scalar2=None, op0=ALU.max)
+                    rest = y[:, lo + V_COLS - LAP : GROUP * U]
+                else:
+                    nc.gpsimd.tensor_copy(out=probe[:, 0:1], in_=newest[0][:, 0:1])
+                    rest = y[:, lo : GROUP * U]
                 nc.gpsimd.tensor_scalar(out=rest, in0=rest, scalar1=FLT_MAX, scalar2=0.0, op0=ALU.min, op1=ALU.max)
                 store(y, first, g_slots[0], GROUP)
             for dst, src in late_copies:

@@ -28,6 +28,7 @@ HEAD_T = 2
 S_COLS = 0
 LOADS = ["w1", (0, 1), (1, 2), "w2", (2, 3), (3, 4), (4, 5), (5, 6), (6, 7), (7, 8), (8, 12), (12, 16)]
 W2_STEP = 0
+ONE_POOL = 1
 S_INTERLEAVES = ()
 FIRST_PLAN = "SSSS"
 BIAS_LATE = True
@@ -62,8 +63,10 @@ def tile_sparsefactorisationdense_pa_t_kernel(tc, h0, k1, k2, m1, m2, scaling, b
         stage = ctx.enter_context(tc.tile_pool(name="stage", bufs=4))
         quant = ctx.enter_context(tc.tile_pool(name="quant", bufs=5))
         ypool = ctx.enter_context(tc.tile_pool(name="ypool", bufs=6))
-        s1pool = ctx.enter_context(tc.psum_pool(name="s1pool", bufs=3))
-        xpool = ctx.enter_context(tc.psum_pool(name="xpool", bufs=5))
+        s1pool = None
+        if ONE_POOL == 0:
+            s1pool = ctx.enter_context(tc.psum_pool(name="s1pool", bufs=3))
+        xpool = ctx.enter_context(tc.psum_pool(name="xpool", bufs=8))
         ctx.enter_context(tc.manual_schedule())
 
         h0v = h0.rearrange("(p j) k -> p (j k)", j=TILES)
@@ -194,7 +197,10 @@ def tile_sparsefactorisationdense_pa_t_kernel(tc, h0, k1, k2, m1, m2, scaling, b
                 g1v = g1_of[g][:].rearrange("p (j r t) -> p j r t", j=GROUP, t=4)
             codes, scales = q0_of[g]
             w1c, w1s = w_q["w1"]
-            s1 = s1pool.tile([P, 4, P], F32, name="s1", tag="s1")
+            if ONE_POOL:
+                s1 = xpool.tile([P, 4, P], F32, name="s1", tag="x")
+            else:
+                s1 = s1pool.tile([P, 4, P], F32, name="s1", tag="s1")
             cols = slice(jj * P, (jj + 1) * P)
             for t in range(4):
                 wcols = slice(t * P, (t + 1) * P)

@@ -25,35 +25,22 @@ L2 = 6
 LAG_A = 3
 LAG_C = 2
 HEAD_T = 2
-S_COLS = 0
-LOADS = ["w1", (0, 1), (1, 2), "w2", (2, 3), (3, 4), (4, 5), (5, 6), (6, 7), (7, 8), (8, 12), (12, 16)]
-W2_STEP = 0
-ONE_POOL = 1
-S_INTERLEAVES = ()
-FIRST_PLAN = "SSSS"
-BIAS_LATE = True
-S_QUEUE = False
-T_PAIRS = False
-HEAD_DEFER = ()
-BIAS_ON_S = False
-FUSED = False
-DEFER = "c0" in "a0 b0 a1 b1 a2 b2 a3 b3 t0 t1"
-V_ORDER = "F C"
-E_BLOCK = 0
-V_COLS = 256
+WARM = 10
+WARM_MID = 2
+V_COLS = 64
 LAP = 8
-STEP_ORDER = "a0 b0 a1 b1 a2 b2 a3 b3 t0 t1"
-RS_LAG = 4
-STORE_TILES = 1
+RS_LAG = 2
+W2_AFTER = "q0(1)"
 NSTEPS = NG + (L2 + GROUP - 1) // GROUP
-
-
-def vector_takes(g, h):
-    return g in (3, 4)
+LATE = ()
+PLANS = ["GGGG", "STTT", "STTT", "STTT", "STST", "STST"]
+LOADS = ["w1", (0, 2), (2, 4), (4, 8), "w2", (8, 12), (12, 16), (16, 20), (20, 24), (24, 28), (28, 32), (32, 48), (48, 64)]
+SPLIT_W1 = True
+HALF_Q0 = True
 
 
 def relu_plan(st):
-    return "STST" if st >= NG else ("SSSS" if st >= NG - 1 else ("SGGG" if st >= NG - LAG_A else "GGGG"))
+    return PLANS[max(0, st - (NG - 4))] if st >= NG - 4 else "GGGG"
 
 
 def tile_sparsefactorisationdense_pa_t_kernel(tc, h0, k1, k2, m1, m2, scaling, bias, out):
@@ -63,9 +50,6 @@ def tile_sparsefactorisationdense_pa_t_kernel(tc, h0, k1, k2, m1, m2, scaling, b
         stage = ctx.enter_context(tc.tile_pool(name="stage", bufs=4))
         quant = ctx.enter_context(tc.tile_pool(name="quant", bufs=5))
         ypool = ctx.enter_context(tc.tile_pool(name="ypool", bufs=6))
-        s1pool = None
-        if ONE_POOL == 0:
-            s1pool = ctx.enter_context(tc.psum_pool(name="s1pool", bufs=3))
         xpool = ctx.enter_context(tc.psum_pool(name="xpool", bufs=8))
         ctx.enter_context(tc.manual_schedule())
 
@@ -74,15 +58,15 @@ def tile_sparsefactorisationdense_pa_t_kernel(tc, h0, k1, k2, m1, m2, scaling, b
 
         brow = const.tile([P, U + 64], BF16, name="brow")
         ones = const.tile([P, P], BF16, name="ones")
-        nc.vector.memset(brow[:], 0.0)
+        zeros = const.tile([P, U], BF16, name="zeros")
         nc.vector.memset(ones[:], 1.0)
+        nc.vector.memset(zeros[:], 0.0)
+        nc.vector.memset(brow[:], 0.0)
         warm = const.tile([P, 8], F32, name="warm")
         nc.vector.memset(warm[:], 0.0)
         nc.scalar.dma_start(out=brow[0:1, 0:U], in_=bias.rearrange("(o n) -> o n", o=1))
         nc.scalar.dma_start(out=brow[0:1, U : U + 1], in_=scaling.rearrange("(o n) -> o n", o=1))
         nc.scalar.activation(out=warm[:], in_=warm[:], func=ACT.Relu)
-        probe = const.tile([P, 8], U32, name="probe")
-        newest = [None]
         ident = const.tile([P, P], F32, name="ident")
         masks.make_identity(nc, ident[:])
 
@@ -90,78 +74,68 @@ def tile_sparsefactorisationdense_pa_t_kernel(tc, h0, k1, k2, m1, m2, scaling, b
         tile_src = {}
         for item in LOADS:
             if item in ("w1", "w2"):
+                pair = []
                 for name, src in (("k", k1 if item == "w1" else k2), ("m", m1 if item == "w1" else m2)):
                     t = const.tile([P, 4 * U], BF16, name=name + item)
-                    nc.sync.dma_start(out=t[:], in_=src.rearrange("(p j) c -> p (j c)", j=4))
                     w_sb[name + item] = t
+                    pair.append((t, src.rearrange("(p j) c -> p (j c)", j=4)))
+                cuts = [(0, 2 * U), (2 * U, 4 * U)] if SPLIT_W1 and item == "w1" else [(0, 4 * U)]
+                for a, b in cuts:
+                    for t, v in pair:
+                        nc.sync.dma_start(out=t[:, a:b], in_=v[:, a:b])
             else:
-                t_a, t_b = 4 * item[0], 4 * item[1]
+                t_a, t_b = item
                 t = const.tile([P, (t_b - t_a) * U], BF16, name="h0t%d" % t_a)
                 nc.sync.dma_start(out=t[:], in_=h0v[:, t_a * U : t_b * U])
                 for i in range(t_a, t_b):
                     tile_src[i] = (t, i - t_a)
 
-        bias_f = const.tile([P, U], F32, name="bias_f")
-        gain_f = const.tile([P, 1], F32, name="gain_f")
+        dps = xpool.tile([P, U], F32, name="dps", tag="x")
 
-        bias_copies = []
+        def dummies(n):
+            for i in range(n):
+                nc.tensor.matmul(out=dps[:], lhsT=ones[:], rhs=zeros[:], start=True, stop=True)
+
+        bias_f = const.tile([P, U + 64], BF16, name="bias_f")
 
         def spread_bias():
-            bias_ps = xpool.tile([P, U], F32, name="bias_ps", tag="x")
-            nc.tensor.matmul(out=bias_ps[:], lhsT=ones[:], rhs=brow[:, 0:U], start=True, stop=True)
-            if BIAS_LATE:
-                bias_copies.append((bias_f[:], bias_ps[:]))
-            elif BIAS_ON_S:
-                nc.scalar.copy(out=bias_f[:], in_=bias_ps[:])
-            else:
-                nc.vector.tensor_copy(out=bias_f[:], in_=bias_ps[:])
-            gain_ps = xpool.tile([P, U], F32, name="gain_ps", tag="x")
-            nc.tensor.matmul(out=gain_ps[:, 0:64], lhsT=ones[:], rhs=brow[:, U : U + 64], start=True, stop=True)
-            if BIAS_LATE:
-                bias_copies.append((gain_f[:], gain_ps[:, 0:1]))
-            elif BIAS_ON_S:
-                nc.scalar.copy(out=gain_f[:], in_=gain_ps[:, 0:1])
-            else:
-                nc.vector.tensor_copy(out=gain_f[:], in_=gain_ps[:, 0:1])
+            bias_ps = xpool.tile([P, 2 * U], BF16, name="bias_ps", tag="x")
+            nc.tensor.matmul(out=bias_ps[:, 0:U], lhsT=ones[:], rhs=brow[:, 0:U], start=True, stop=True)
+            nc.tensor.matmul(out=bias_ps[:, U : U + 64], lhsT=ones[:], rhs=brow[:, U : U + 64], start=True, stop=True)
+            return bias_ps
 
-        def quantise(src, name, pool, width=GCOLS):
+        def quantise_into(codes, scales, src, a, b):
+            nc.vector.quantize_mx(out=codes[:, a:b].bitcast(FP8X4), scales=scales[:, a:b], in_=src[:, 4 * a : 4 * b])
+
+        def quantised(name, pool, width=GCOLS):
             codes = pool.tile([P, width], U32, name=name + "_c", tag=name + "_c", align_bytes=64)
             scales = pool.tile([P, width], U8, name=name + "_s", tag=name + "_s", align_bytes=64)
-            nc.vector.quantize_mx(out=codes[:].bitcast(FP8X4), scales=scales[:], in_=src[:])
-            newest[0] = codes
             return codes, scales
 
         def prepare_w(item):
             kk, mm = w_sb["k" + item], w_sb["m" + item]
             grouped = const.tile([P, 4 * U], BF16, name=item + "g", align_bytes=64)
-            dst_view = "p (s q t) -> p s q t" if item == "w1" else "p (s q t) -> p q s t"
-            dst = grouped[:].rearrange(dst_view, s=4 if item == "w1" else 1, t=4)
-            src_view = "p (t q s) -> p s q t" if item == "w1" else "p (t q s) -> p q s t"
-            if FUSED:
-                nc.vector.tensor_tensor(
-                    out=dst,
-                    in0=kk[:].rearrange(src_view, t=4, s=4 if item == "w1" else 1),
-                    in1=mm[:].rearrange(src_view, t=4, s=4 if item == "w1" else 1),
-                    op=ALU.mult,
-                )
+            codes, scales = quantised(item, const, U)
+            for a in (0, 2 * U):
+                nc.vector.tensor_tensor(out=kk[:, a : a + 2 * U], in0=kk[:, a : a + 2 * U], in1=mm[:, a : a + 2 * U], op=ALU.mult)
+            if item == "w1":
+                dst = grouped[:].rearrange("p (s q t) -> p s q t", s=4, t=4)
+                src = kk[:].rearrange("p (t q s) -> p s q t", t=4, s=4)
+                for s in (0, 2):
+                    nc.vector.tensor_copy(out=dst[:, s : s + 2], in_=src[:, s : s + 2])
             else:
-                nc.vector.tensor_tensor(out=kk[:], in0=kk[:], in1=mm[:], op=ALU.mult)
-                if item in S_INTERLEAVES:
-                    nc.scalar.copy(out=dst, in_=kk[:].rearrange(src_view, t=4, s=4 if item == "w1" else 1))
-                else:
-                    nc.vector.tensor_copy(out=dst, in_=kk[:].rearrange(src_view, t=4, s=4 if item == "w1" else 1))
-            return quantise(grouped, item, const, U)
+                dst = grouped[:].rearrange("p (q t) -> p q t", t=4)
+                src = kk[:].rearrange("p (t q) -> p q t", t=4)
+                for s in (0, U // 2):
+                    nc.vector.tensor_copy(out=dst[:, s : s + U // 2], in_=src[:, s : s + U // 2])
+            for a in (0, U // 2):
+                quantise_into(codes, scales, grouped, a, a + U // 2)
+            return codes, scales
 
+        g0_of, q0_of, g1_of, q1_of, w_q = {}, {}, {}, {}, {}
         late_copies = []
-        held = {}
-        g0_of = {}
-        q0_of = {}
-        g1_of = {}
-        q1_of = {}
-        y_of = {}
-        w_q = {}
 
-        def transpose_bank(g, h, defer=False):
+        def transpose_bank(g, h):
             if h == 0:
                 g0_of[g] = stage.tile([P, 4 * GCOLS], BF16, name="g0", tag="g0", align_bytes=64)
             g0w = g0_of[g][:].bitcast(F32).rearrange("p (j r u) -> p j r u", j=GROUP, u=2)
@@ -173,34 +147,24 @@ def tile_sparsefactorisationdense_pa_t_kernel(tc, h0, k1, k2, m1, m2, scaling, b
                     w0 = i * (U // 2)
                     nc.tensor.transpose(tp[:, jj, u, :], words[:, w0 + u : w0 + U // 2 : 2], ident[:])
             pair = (g0w[:, 2 * h : 2 * h + 2, :, :], tp[:].rearrange("p j u r -> p j r u"))
-            if vector_takes(g, h):
+            if g in LATE:
                 late_copies.append(pair)
-            elif defer:
-                assert held.get(h) is None
-                held[h] = pair
             else:
                 nc.scalar.copy(out=pair[0], in_=pair[1])
 
-        def transposes(g, defer=False):
-            for h in range(GROUP // 2):
-                transpose_bank(g, h, defer)
-
-        def quantise_h0(g):
-            q0_of[g] = quantise(g0_of[g], "q0", quant)
+        def quantise_h0(g, halves=1):
+            q0_of[g] = quantised("q0", quant)
+            w = GCOLS // halves
+            for i in range(halves):
+                quantise_into(q0_of[g][0], q0_of[g][1], g0_of[g], i * w, (i + 1) * w)
 
         def stage1(g, jj):
             if jj == 0:
                 g1_of[g] = stage.tile([P, 4 * GCOLS], BF16, name="g1", tag="g1", align_bytes=64)
-            if E_BLOCK:
-                g1v = g1_of[g][:].rearrange("p (j c i t) -> p j c t i", j=GROUP, i=E_BLOCK, t=4)
-            else:
-                g1v = g1_of[g][:].rearrange("p (j r t) -> p j r t", j=GROUP, t=4)
+            g1v = g1_of[g][:].rearrange("p (j r t) -> p j r t", j=GROUP, t=4)
             codes, scales = q0_of[g]
             w1c, w1s = w_q["w1"]
-            if ONE_POOL:
-                s1 = xpool.tile([P, 4, P], F32, name="s1", tag="x")
-            else:
-                s1 = s1pool.tile([P, 4, P], F32, name="s1", tag="s1")
+            s1 = xpool.tile([P, 4, P], F32, name="s1", tag="x")
             cols = slice(jj * P, (jj + 1) * P)
             for t in range(4):
                 wcols = slice(t * P, (t + 1) * P)
@@ -213,19 +177,18 @@ def tile_sparsefactorisationdense_pa_t_kernel(tc, h0, k1, k2, m1, m2, scaling, b
                     start=True,
                     stop=True,
                 )
-            if E_BLOCK:
-                nc.scalar.copy(out=g1v[:, jj], in_=s1[:].rearrange("p t (c i) -> p c t i", i=E_BLOCK))
-            else:
-                nc.scalar.copy(out=g1v[:, jj, :, :], in_=s1[:].rearrange("p t r -> p r t"))
+            nc.scalar.copy(out=g1v[:, jj, :, :], in_=s1[:].rearrange("p t r -> p r t"))
 
-        def quantise_h1(g):
-            q1_of[g] = quantise(g1_of[g], "q1", quant)
+        def quantise_h1(g, halves=1):
+            q1_of[g] = quantised("q1", quant)
+            w = GCOLS // halves
+            for i in range(halves):
+                quantise_into(q1_of[g][0], q1_of[g][1], g1_of[g], i * w, (i + 1) * w)
 
         def stage2(tile_no, y, slot):
             codes, scales = q1_of[tile_no // GROUP]
             w2c, w2s = w_q["w2"]
-            jj = tile_no % GROUP
-            cols = slice(jj * P, (jj + 1) * P)
+            cols = slice((tile_no % GROUP) * P, (tile_no % GROUP + 1) * P)
             s2 = xpool.tile([P, U], F32, name="s2", tag="x")
             nc.tensor.matmul_mx(
                 out=s2[:],
@@ -239,8 +202,8 @@ def tile_sparsefactorisationdense_pa_t_kernel(tc, h0, k1, k2, m1, m2, scaling, b
             nc.vector.scalar_tensor_tensor(
                 out=y[:, slot * U : (slot + 1) * U],
                 in0=s2[:],
-                scalar=gain_f[:, 0:1],
-                in1=bias_f[:],
+                scalar=bias_f[:, U : U + 1],
+                in1=bias_f[:, 0:U],
                 op0=ALU.mult,
                 op1=ALU.add,
             )
@@ -248,32 +211,44 @@ def tile_sparsefactorisationdense_pa_t_kernel(tc, h0, k1, k2, m1, m2, scaling, b
         def relu_scalar(y, a, b):
             nc.scalar.activation(out=y[:, a:b], in_=y[:, a:b], func=ACT.Relu)
 
-        def store(y, first_tile, slot_a, slot_b, queue=None):
-            (queue or nc.sync).dma_start(
+        def relu_gpsimd(y, a, b):
+            nc.gpsimd.tensor_scalar(out=y[:, a:b], in0=y[:, a:b], scalar1=FLT_MAX, scalar2=0.0, op0=ALU.min, op1=ALU.max)
+
+        def store(y, first_tile, slot_a, slot_b):
+            nc.sync.dma_start(
                 out=outv[:, first_tile + slot_a : first_tile + slot_b, :],
                 in_=y[:, slot_a * U : slot_b * U].rearrange("p (j n) -> p j n", n=U),
             )
 
-        if BIAS_ON_S:
-            spread_bias()
+        dummies(WARM)
         w_q["w1"] = prepare_w("w1")
         for g in range(HEAD_T):
-            transposes(g)
+            for h in range(2):
+                transpose_bank(g, h)
+            if WARM_MID:
+                dummies(WARM_MID)
+            if g == 0:
+                quantise_h0(0, 2 if HALF_Q0 else 1)
+        bias_ps = None
+        if W2_AFTER == "q0(0)":
+            w_q["w2"] = prepare_w("w2")
+        for g in range(1, HEAD_T):
             quantise_h0(g)
-        if not BIAS_ON_S:
-            spread_bias()
+        if W2_AFTER == "q0(1)":
+            w_q["w2"] = prepare_w("w2")
         next_c = HEAD_T
         for st in range(NSTEPS):
             first = GROUP * st - L2
             slots = [jj for jj in range(GROUP) if 0 <= first + jj < TILES]
-            plan = relu_plan(st) if len(slots) == GROUP else (FIRST_PLAN if st < NG else "S" * GROUP)
+            plan = relu_plan(st)
+            if len(slots) < GROUP and st < NG:
+                plan = "GGGG"
             g_slots = [jj for jj in slots if plan[jj] == "G"]
             t_slots = [jj for jj in slots if plan[jj] != "G"]
             y = None
             if slots:
                 y = ypool.tile([P, GROUP * U], F32, name="y", tag="y")
             waiting = []
-            unsaved = []
 
             def tile_relus(upto):
                 for s in [w for w in waiting if w <= upto]:
@@ -281,61 +256,46 @@ def tile_sparsefactorisationdense_pa_t_kernel(tc, h0, k1, k2, m1, m2, scaling, b
                     if plan[s] == "S":
                         relu_scalar(y, s * U, (s + 1) * U)
                     else:
-                        ap = y[:, s * U : (s + 1) * U]
-                        nc.gpsimd.tensor_scalar(out=ap, in0=ap, scalar1=FLT_MAX, scalar2=0.0, op0=ALU.min, op1=ALU.max)
-                    unsaved.append(s)
-                    if len(unsaved) == STORE_TILES or s == t_slots[-1]:
-                        store(y, first, unsaved[0], unsaved[-1] + 1, nc.scalar if S_QUEUE and plan[s] == "S" else None)
-                        unsaved.clear()
+                        relu_gpsimd(y, s * U, (s + 1) * U)
+                    store(y, first, s, s + 1)
 
-            for word in STEP_ORDER.split():
-                jj = int(word[1])
-                if word[0] == "a" and st < NG:
+            for jj in range(GROUP):
+                if st < NG:
                     stage1(st, jj)
                     tile_relus(jj - RS_LAG)
-                if word[0] == "b" and jj in slots:
+                if jj in slots:
                     stage2(first + jj, y, jj)
-                    if jj in t_slots:
+                    if plan[jj] == "T":
+                        relu_gpsimd(y, jj * U, (jj + 1) * U)
+                        store(y, first, jj, jj + 1)
+                    elif jj in t_slots:
                         waiting.append(jj)
                     if st >= NG:
                         tile_relus(jj)
-                if word[0] == "t" and 0 < st and st + LAG_A < NG:
-                    transpose_bank(st + LAG_A, jj, DEFER)
-                if word[0] == "c" and held.get(jj) is not None:
-                    nc.scalar.copy(out=held[jj][0], in_=held[jj][1])
-                    held[jj] = None
             if st == 0:
+                bias_ps = spread_bias()
                 for g in range(HEAD_T, LAG_A + 1):
-                    for h in range(GROUP // 2):
-                        transpose_bank(g, h, g == LAG_A and h in HEAD_DEFER)
-                for dst, src in bias_copies:
-                    nc.scalar.copy(out=dst, in_=src)
-            elif T_PAIRS and st % 2 == 1:
-                for g in (st + LAG_A, st + LAG_A + 1):
-                    if g < NG:
-                        transposes(g)
+                    for h in range(2):
+                        transpose_bank(g, h)
+                    if g == HEAD_T:
+                        nc.scalar.copy(out=bias_f[:, 0 : U + 2], in_=bias_ps[:, 0 : U + 2])
+            elif st + LAG_A < NG:
+                for h in range(2):
+                    transpose_bank(st + LAG_A, h)
             tile_relus(GROUP)
-            if st == W2_STEP:
+            if W2_AFTER == st:
                 w_q["w2"] = prepare_w("w2")
-            if g_slots and not t_slots and S_COLS:
-                relu_scalar(y, 0, S_COLS)
-            for word in V_ORDER.split():
-                if word == "F" and st < NG:
-                    quantise_h1(st)
-                while word == "C" and next_c < NG and next_c <= st + LAG_C:
-                    quantise_h0(next_c)
-                    next_c += 1
+            if st < NG:
+                quantise_h1(st)
+            while next_c < NG and next_c <= st + LAG_C:
+                quantise_h0(next_c)
+                next_c += 1
             if g_slots:
-                lo = g_slots[0] * U + (0 if t_slots else S_COLS)
-                if V_COLS:
-                    mine = y[:, lo : lo + V_COLS]
-                    nc.vector.tensor_scalar(out=mine, in0=mine, scalar1=0.0, scalar2=None, op0=ALU.max)
-                    rest = y[:, lo + V_COLS - LAP : GROUP * U]
-                else:
-                    nc.gpsimd.tensor_copy(out=probe[:, 0:1], in_=newest[0][:, 0:1])
-                    rest = y[:, lo : GROUP * U]
-                nc.gpsimd.tensor_scalar(out=rest, in0=rest, scalar1=FLT_MAX, scalar2=0.0, op0=ALU.min, op1=ALU.max)
-                store(y, first, g_slots[0], GROUP)
+                lo = g_slots[0] * U
+                mine = y[:, lo : lo + V_COLS]
+                nc.vector.tensor_scalar(out=mine, in0=mine, scalar1=0.0, scalar2=None, op0=ALU.max)
+                relu_gpsimd(y, lo + V_COLS - LAP, (g_slots[-1] + 1) * U)
+                store(y, first, g_slots[0], g_slots[-1] + 1)
             for dst, src in late_copies:
                 nc.vector.tensor_copy(out=dst, in_=src)
             late_copies.clear()

@@ -27,12 +27,12 @@ LAG_C = 2
 HEAD_T = 2
 WARM = 10
 WARM_MID = 2
-V_COLS = 64
+V_COLS = 256
+S_COLS = 256
 LAP = 8
 RS_LAG = 2
 W2_AFTER = "q0(1)"
 NSTEPS = NG + (L2 + GROUP - 1) // GROUP
-LATE = ()
 PLANS = ["GGGG", "STTT", "STTT", "STTT", "STST", "STST"]
 LOADS = ["w1", (0, 2), (2, 4), (4, 8), "w2", (8, 12), (12, 16), (16, 20), (20, 24), (24, 28), (28, 32), (32, 48), (48, 64)]
 SPLIT_W1 = True
@@ -133,7 +133,6 @@ def tile_sparsefactorisationdense_pa_t_kernel(tc, h0, k1, k2, m1, m2, scaling, b
             return codes, scales
 
         g0_of, q0_of, g1_of, q1_of, w_q = {}, {}, {}, {}, {}
-        late_copies = []
 
         def transpose_bank(g, h):
             if h == 0:
@@ -147,10 +146,7 @@ def tile_sparsefactorisationdense_pa_t_kernel(tc, h0, k1, k2, m1, m2, scaling, b
                     w0 = i * (U // 2)
                     nc.tensor.transpose(tp[:, jj, u, :], words[:, w0 + u : w0 + U // 2 : 2], ident[:])
             pair = (g0w[:, 2 * h : 2 * h + 2, :, :], tp[:].rearrange("p j u r -> p j r u"))
-            if g in LATE:
-                late_copies.append(pair)
-            else:
-                nc.scalar.copy(out=pair[0], in_=pair[1])
+            nc.scalar.copy(out=pair[0], in_=pair[1])
 
         def quantise_h0(g, halves=1):
             q0_of[g] = quantised("q0", quant)
@@ -292,10 +288,9 @@ def tile_sparsefactorisationdense_pa_t_kernel(tc, h0, k1, k2, m1, m2, scaling, b
                 next_c += 1
             if g_slots:
                 lo = g_slots[0] * U
+                relu_scalar(y, lo, lo + S_COLS)
+                lo += S_COLS
                 mine = y[:, lo : lo + V_COLS]
                 nc.vector.tensor_scalar(out=mine, in0=mine, scalar1=0.0, scalar2=None, op0=ALU.max)
                 relu_gpsimd(y, lo + V_COLS - LAP, (g_slots[-1] + 1) * U)
                 store(y, first, g_slots[0], g_slots[-1] + 1)
-            for dst, src in late_copies:
-                nc.vector.tensor_copy(out=dst, in_=src)
-            late_copies.clear()

@@ -25,15 +25,19 @@ L2 = 6
 LAG_A = 3
 LAG_C = 2
 HEAD_T = 2
-WARM = 10
-WARM_MID = 2
 V_COLS = 256
 S_COLS = 256
 LAP = 8
 RS_LAG = 2
-W2_AFTER = "q0(1)"
+HEAD = "D12 T0 D3 T1 Q0h Q1 W"
+TR = {0: (2, 3)}
+Q0 = {0: (2,)}
+BIAS_AT = 0
+QORDER = "10"
+TRPOS = 4
+PAIR = 2
 NSTEPS = NG + (L2 + GROUP - 1) // GROUP
-PLANS = ["GGGG", "STTT", "STTT", "STTT", "STST", "STST"]
+PLANS = ["GGGG", "TTSS", "TTSS", "TTSS", "SSSS", "SSSS"]
 LOADS = ["w1", (0, 2), (2, 4), (4, 8), "w2", (8, 12), (12, 16), (16, 20), (20, 24), (24, 28), (28, 32), (32, 48), (48, 64)]
 SPLIT_W1 = True
 HALF_Q0 = True
@@ -207,6 +211,9 @@ def tile_sparsefactorisationdense_pa_t_kernel(tc, h0, k1, k2, m1, m2, scaling, b
         def relu_scalar(y, a, b):
             nc.scalar.activation(out=y[:, a:b], in_=y[:, a:b], func=ACT.Relu)
 
+        def relu_vector(y, a, b):
+            nc.vector.tensor_scalar(out=y[:, a:b], in0=y[:, a:b], scalar1=0.0, scalar2=None, op0=ALU.max)
+
         def relu_gpsimd(y, a, b):
             nc.gpsimd.tensor_scalar(out=y[:, a:b], in0=y[:, a:b], scalar1=FLT_MAX, scalar2=0.0, op0=ALU.min, op1=ALU.max)
 
@@ -216,23 +223,43 @@ def tile_sparsefactorisationdense_pa_t_kernel(tc, h0, k1, k2, m1, m2, scaling, b
                 in_=y[:, slot_a * U : slot_b * U].rearrange("p (j n) -> p j n", n=U),
             )
 
-        dummies(WARM)
-        w_q["w1"] = prepare_w("w1")
-        for g in range(HEAD_T):
-            for h in range(2):
-                transpose_bank(g, h)
-            if WARM_MID:
-                dummies(WARM_MID)
-            if g == 0:
-                quantise_h0(0, 2 if HALF_Q0 else 1)
-        bias_ps = None
-        if W2_AFTER == "q0(0)":
-            w_q["w2"] = prepare_w("w2")
-        for g in range(1, HEAD_T):
-            quantise_h0(g)
-        if W2_AFTER == "q0(1)":
-            w_q["w2"] = prepare_w("w2")
-        next_c = HEAD_T
+        ready = {}
+
+        def finished(y, first, s):
+            n = 1 if first + GROUP >= TILES else PAIR
+            base = s // n * n
+            ready.setdefault((first, base), set()).add(s)
+            if len(ready[(first, base)]) == n:
+                store(y, first, base, base + n)
+
+        def do_head(script):
+            for tok in script.split():
+                c = tok[0]
+                if c == "D":
+                    dummies(int(tok[1:]))
+                elif c == "T":
+                    for h in range(2):
+                        transpose_bank(int(tok[1:]), h)
+                elif c == "Q":
+                    if tok[-1] == "h":
+                        quantise_h0(int(tok[1:-1]), 2)
+                    else:
+                        quantise_h0(int(tok[1:]))
+                elif c == "W":
+                    w_q["w2"] = prepare_w("w2")
+                elif c == "X":
+                    w_q["w1"] = prepare_w("w1")
+
+        def run_transposes(st):
+            if st == BIAS_AT:
+                bias_ps = spread_bias()
+            for n, g in enumerate(TR.get(st, (st + LAG_A,) if st + LAG_A < NG else ())):
+                for h in range(2):
+                    transpose_bank(g, h)
+                if st == BIAS_AT and n == 0:
+                    nc.scalar.copy(out=bias_f[:, 0 : U + 2], in_=bias_ps[:, 0 : U + 2])
+
+        do_head(HEAD if "X" in HEAD else HEAD.split()[0] + " X " + " ".join(HEAD.split()[1:]))
         for st in range(NSTEPS):
             first = GROUP * st - L2
             slots = [jj for jj in range(GROUP) if 0 <= first + jj < TILES]
@@ -245,47 +272,44 @@ def tile_sparsefactorisationdense_pa_t_kernel(tc, h0, k1, k2, m1, m2, scaling, b
             if slots:
                 y = ypool.tile([P, GROUP * U], F32, name="y", tag="y")
             waiting = []
+            vwait = []
 
             def tile_relus(upto):
                 for s in [w for w in waiting if w <= upto]:
                     waiting.remove(s)
-                    if plan[s] == "S":
-                        relu_scalar(y, s * U, (s + 1) * U)
-                    else:
-                        relu_gpsimd(y, s * U, (s + 1) * U)
-                    store(y, first, s, s + 1)
+                    relu_scalar(y, s * U, (s + 1) * U)
+                    finished(y, first, s)
 
             for jj in range(GROUP):
                 if st < NG:
                     stage1(st, jj)
                     tile_relus(jj - RS_LAG)
+                if jj == TRPOS and st > 0:
+                    run_transposes(st)
                 if jj in slots:
                     stage2(first + jj, y, jj)
-                    if plan[jj] == "T":
+                    for s in vwait:
+                        relu_vector(y, s * U, (s + 1) * U)
+                        finished(y, first, s)
+                    vwait.clear()
+                    if plan[jj] == "V":
+                        vwait.append(jj)
+                    elif plan[jj] == "T":
                         relu_gpsimd(y, jj * U, (jj + 1) * U)
-                        store(y, first, jj, jj + 1)
+                        finished(y, first, jj)
                     elif jj in t_slots:
                         waiting.append(jj)
                     if st >= NG:
                         tile_relus(jj)
-            if st == 0:
-                bias_ps = spread_bias()
-                for g in range(HEAD_T, LAG_A + 1):
-                    for h in range(2):
-                        transpose_bank(g, h)
-                    if g == HEAD_T:
-                        nc.scalar.copy(out=bias_f[:, 0 : U + 2], in_=bias_ps[:, 0 : U + 2])
-            elif st + LAG_A < NG:
-                for h in range(2):
-                    transpose_bank(st + LAG_A, h)
+            if TRPOS == 4 or st == 0:
+                run_transposes(st)
             tile_relus(GROUP)
-            if W2_AFTER == st:
-                w_q["w2"] = prepare_w("w2")
-            if st < NG:
-                quantise_h1(st)
-            while next_c < NG and next_c <= st + LAG_C:
-                quantise_h0(next_c)
-                next_c += 1
+            for c in QORDER:
+                if c == "1" and st < NG:
+                    quantise_h1(st)
+                if c == "0":
+                    for g in Q0.get(st, (st + LAG_C,) if st + LAG_C < NG else ()):
+                        quantise_h0(g)
             if g_slots:
                 lo = g_slots[0] * U
                 relu_scalar(y, lo, lo + S_COLS)

@@ -71,7 +71,7 @@ def tile_sparsefactorisationdense_pa_t_kernel(tc, h0, k1, k2, m1, m2, scaling, b
         nc.scalar.dma_start(out=brow[0:1, 0:U], in_=bias.rearrange("(o n) -> o n", o=1))
         nc.scalar.dma_start(out=brow[0:1, U : U + 1], in_=scaling.rearrange("(o n) -> o n", o=1))
         nc.scalar.activation(out=warm[:], in_=warm[:], func=ACT.Relu)
-        ident = const.tile([P, P], F32, name="ident")
+        ident = const.tile([P, P], F32, name="ident", align_bytes=256)
         masks.make_identity(nc, ident[:])
 
         w_sb = {}
@@ -89,7 +89,7 @@ def tile_sparsefactorisationdense_pa_t_kernel(tc, h0, k1, k2, m1, m2, scaling, b
                         nc.sync.dma_start(out=t[:, a:b], in_=v[:, a:b])
             else:
                 t_a, t_b = item
-                t = const.tile([P, (t_b - t_a) * U], BF16, name="h0t%d" % t_a)
+                t = const.tile([P, (t_b - t_a) * U], BF16, name="h0t%d" % t_a, align_bytes=256)
                 nc.sync.dma_start(out=t[:], in_=h0v[:, t_a * U : t_b * U])
                 for i in range(t_a, t_b):
                     tile_src[i] = (t, i - t_a)
@@ -112,13 +112,13 @@ def tile_sparsefactorisationdense_pa_t_kernel(tc, h0, k1, k2, m1, m2, scaling, b
             nc.vector.quantize_mx(out=codes[:, a:b].bitcast(FP8X4), scales=scales[:, a:b], in_=src[:, 4 * a : 4 * b])
 
         def quantised(name, pool, width=GCOLS):
-            codes = pool.tile([P, width], U32, name=name + "_c", tag=name + "_c", align_bytes=64)
-            scales = pool.tile([P, width], U8, name=name + "_s", tag=name + "_s", align_bytes=64)
+            codes = pool.tile([P, width], U32, name=name + "_c", tag=name + "_c", align_bytes=256)
+            scales = pool.tile([P, width], U8, name=name + "_s", tag=name + "_s", align_bytes=256)
             return codes, scales
 
         def prepare_w(item):
             kk, mm = w_sb["k" + item], w_sb["m" + item]
-            grouped = const.tile([P, 4 * U], BF16, name=item + "g", align_bytes=64)
+            grouped = const.tile([P, 4 * U], BF16, name=item + "g", align_bytes=256)
             codes, scales = quantised(item, const, U)
             for a in (0, 2 * U):
                 nc.vector.tensor_tensor(out=kk[:, a : a + 2 * U], in0=kk[:, a : a + 2 * U], in1=mm[:, a : a + 2 * U], op=ALU.mult)
@@ -140,7 +140,7 @@ def tile_sparsefactorisationdense_pa_t_kernel(tc, h0, k1, k2, m1, m2, scaling, b
 
         def transpose_bank(g, h):
             if h == 0:
-                g0_of[g] = stage.tile([P, 4 * GCOLS], BF16, name="g0", tag="g0", align_bytes=64)
+                g0_of[g] = stage.tile([P, 4 * GCOLS], BF16, name="g0", tag="g0", align_bytes=256)
             g0w = g0_of[g][:].bitcast(F32).rearrange("p (j r u) -> p j r u", j=GROUP, u=2)
             tp = xpool.tile([P, 2, 2, P], F32, name="tp", tag="x")
             for jj in range(2):
@@ -160,7 +160,7 @@ def tile_sparsefactorisationdense_pa_t_kernel(tc, h0, k1, k2, m1, m2, scaling, b
 
         def stage1(g, jj):
             if jj == 0:
-                g1_of[g] = stage.tile([P, 4 * GCOLS], BF16, name="g1", tag="g1", align_bytes=64)
+                g1_of[g] = stage.tile([P, 4 * GCOLS], BF16, name="g1", tag="g1", align_bytes=256)
             g1v = g1_of[g][:].rearrange("p (j r t) -> p j r t", j=GROUP, t=4)
             codes, scales = q0_of[g]
             w1c, w1s = w_q["w1"]

@@ -25,26 +25,23 @@ L2 = 6
 LAG_A = 3
 LAG_C = 2
 HEAD_T = 2
+SORTED = (4, 5)
+WARM = (12, 3, 2)
 V_COLS = 256
 S_COLS = 256
+S_FROM = 3
 LAP = 8
-RS_LAG = 2
-HEAD = "D12 T0 D3 T1 Q0h Q1 W"
-TR = {0: (2, 3)}
-Q0 = {0: (2,)}
-BIAS_AT = 0
-QORDER = "10"
-TRPOS = 4
-PAIR = 2
+RS_LAG = 3
 NSTEPS = NG + (L2 + GROUP - 1) // GROUP
-PLANS = ["GGGG", "TTSS", "TTSS", "TTSS", "SSSS", "SSSS"]
 LOADS = ["w1", (0, 2), (2, 4), (4, 8), "w2", (8, 12), (12, 16), (16, 20), (20, 24), (24, 28), (28, 32), (32, 48), (48, 64)]
-SPLIT_W1 = True
-HALF_Q0 = True
 
 
 def relu_plan(st):
-    return PLANS[max(0, st - (NG - 4))] if st >= NG - 4 else "GGGG"
+    if st >= NG:
+        return "SSSS"
+    if st > NG - LAG_A:
+        return "TTSS"
+    return "SSGG" if st == NG - LAG_A else "GGGG"
 
 
 def tile_sparsefactorisationdense_pa_t_kernel(tc, h0, k1, k2, m1, m2, scaling, bias, out):
@@ -83,10 +80,9 @@ def tile_sparsefactorisationdense_pa_t_kernel(tc, h0, k1, k2, m1, m2, scaling, b
                     t = const.tile([P, 4 * U], BF16, name=name + item)
                     w_sb[name + item] = t
                     pair.append((t, src.rearrange("(p j) c -> p (j c)", j=4)))
-                cuts = [(0, 2 * U), (2 * U, 4 * U)] if SPLIT_W1 and item == "w1" else [(0, 4 * U)]
-                for a, b in cuts:
+                for a in (0, 2 * U):
                     for t, v in pair:
-                        nc.sync.dma_start(out=t[:, a:b], in_=v[:, a:b])
+                        nc.sync.dma_start(out=t[:, a : a + 2 * U], in_=v[:, a : a + 2 * U])
             else:
                 t_a, t_b = item
                 t = const.tile([P, (t_b - t_a) * U], BF16, name="h0t%d" % t_a, align_bytes=256)
@@ -116,12 +112,15 @@ def tile_sparsefactorisationdense_pa_t_kernel(tc, h0, k1, k2, m1, m2, scaling, b
             scales = pool.tile([P, width], U8, name=name + "_s", tag=name + "_s", align_bytes=256)
             return codes, scales
 
-        def prepare_w(item):
-            kk, mm = w_sb["k" + item], w_sb["m" + item]
+        def product(item, half):
+            ks = w_sb["k" + item][:, half * 2 * U : (half + 1) * 2 * U]
+            ms = w_sb["m" + item][:, half * 2 * U : (half + 1) * 2 * U]
+            nc.vector.tensor_tensor(out=ks, in0=ks, in1=ms, op=ALU.mult)
+
+        def quantise_w(item):
+            kk = w_sb["k" + item]
             grouped = const.tile([P, 4 * U], BF16, name=item + "g", align_bytes=256)
             codes, scales = quantised(item, const, U)
-            for a in (0, 2 * U):
-                nc.vector.tensor_tensor(out=kk[:, a : a + 2 * U], in0=kk[:, a : a + 2 * U], in1=mm[:, a : a + 2 * U], op=ALU.mult)
             if item == "w1":
                 dst = grouped[:].rearrange("p (s q t) -> p s q t", s=4, t=4)
                 src = kk[:].rearrange("p (t q s) -> p s q t", t=4, s=4)
@@ -137,6 +136,16 @@ def tile_sparsefactorisationdense_pa_t_kernel(tc, h0, k1, k2, m1, m2, scaling, b
             return codes, scales
 
         g0_of, q0_of, g1_of, q1_of, w_q = {}, {}, {}, {}, {}
+        sorted_of = {}
+
+        def sort_words(g, h):
+            src, i = tile_src[g * GROUP + 2 * h]
+            t = const.tile([P, 2 * U], BF16, name="sorted%d_%d" % (g, h), align_bytes=256)
+            nc.vector.tensor_copy(
+                out=t[:].bitcast(F32).rearrange("p (j u w) -> p j u w", j=2, u=2),
+                in_=src[:, i * U : (i + 2) * U].bitcast(F32).rearrange("p (j w u) -> p j u w", j=2, u=2),
+            )
+            sorted_of[g, h] = t
 
         def transpose_bank(g, h):
             if h == 0:
@@ -145,17 +154,20 @@ def tile_sparsefactorisationdense_pa_t_kernel(tc, h0, k1, k2, m1, m2, scaling, b
             tp = xpool.tile([P, 2, 2, P], F32, name="tp", tag="x")
             for jj in range(2):
                 src, i = tile_src[g * GROUP + 2 * h + jj]
-                words = src[:].bitcast(F32)
                 for u in range(2):
-                    w0 = i * (U // 2)
-                    nc.tensor.transpose(tp[:, jj, u, :], words[:, w0 + u : w0 + U // 2 : 2], ident[:])
-            pair = (g0w[:, 2 * h : 2 * h + 2, :, :], tp[:].rearrange("p j u r -> p j r u"))
-            nc.scalar.copy(out=pair[0], in_=pair[1])
+                    if g in SORTED:
+                        w0 = (2 * jj + u) * P
+                        words = sorted_of[g, h][:].bitcast(F32)[:, w0 : w0 + P]
+                    else:
+                        w0 = i * (U // 2)
+                        words = src[:].bitcast(F32)[:, w0 + u : w0 + U // 2 : 2]
+                    nc.tensor.transpose(tp[:, jj, u, :], words, ident[:])
+            nc.scalar.copy(out=g0w[:, 2 * h : 2 * h + 2, :, :], in_=tp[:].rearrange("p j u r -> p j r u"))
 
-        def quantise_h0(g, halves=1):
+        def quantise_h0(g, pieces=1):
             q0_of[g] = quantised("q0", quant)
-            w = GCOLS // halves
-            for i in range(halves):
+            w = GCOLS // pieces
+            for i in range(pieces):
                 quantise_into(q0_of[g][0], q0_of[g][1], g0_of[g], i * w, (i + 1) * w)
 
         def stage1(g, jj):
@@ -179,11 +191,9 @@ def tile_sparsefactorisationdense_pa_t_kernel(tc, h0, k1, k2, m1, m2, scaling, b
                 )
             nc.scalar.copy(out=g1v[:, jj, :, :], in_=s1[:].rearrange("p t r -> p r t"))
 
-        def quantise_h1(g, halves=1):
+        def quantise_h1(g):
             q1_of[g] = quantised("q1", quant)
-            w = GCOLS // halves
-            for i in range(halves):
-                quantise_into(q1_of[g][0], q1_of[g][1], g1_of[g], i * w, (i + 1) * w)
+            quantise_into(q1_of[g][0], q1_of[g][1], g1_of[g], 0, GCOLS)
 
         def stage2(tile_no, y, slot):
             codes, scales = q1_of[tile_no // GROUP]
@@ -211,9 +221,6 @@ def tile_sparsefactorisationdense_pa_t_kernel(tc, h0, k1, k2, m1, m2, scaling, b
         def relu_scalar(y, a, b):
             nc.scalar.activation(out=y[:, a:b], in_=y[:, a:b], func=ACT.Relu)
 
-        def relu_vector(y, a, b):
-            nc.vector.tensor_scalar(out=y[:, a:b], in0=y[:, a:b], scalar1=0.0, scalar2=None, op0=ALU.max)
-
         def relu_gpsimd(y, a, b):
             nc.gpsimd.tensor_scalar(out=y[:, a:b], in0=y[:, a:b], scalar1=FLT_MAX, scalar2=0.0, op0=ALU.min, op1=ALU.max)
 
@@ -223,97 +230,84 @@ def tile_sparsefactorisationdense_pa_t_kernel(tc, h0, k1, k2, m1, m2, scaling, b
                 in_=y[:, slot_a * U : slot_b * U].rearrange("p (j n) -> p j n", n=U),
             )
 
-        ready = {}
+        dummies(WARM[0])
+        for half in range(2):
+            product("w1", half)
+        w_q["w1"] = quantise_w("w1")
+        for g in range(HEAD_T):
+            for h in range(2):
+                transpose_bank(g, h)
+            if g == 0:
+                dummies(WARM[1])
+        quantise_h0(0, 2)
+        product("w2", 0)
+        quantise_h0(1)
+        product("w2", 1)
+        w_q["w2"] = quantise_w("w2")
 
-        def finished(y, first, s):
-            n = 1 if first + GROUP >= TILES else PAIR
-            base = s // n * n
-            ready.setdefault((first, base), set()).add(s)
-            if len(ready[(first, base)]) == n:
-                store(y, first, base, base + n)
-
-        def do_head(script):
-            for tok in script.split():
-                c = tok[0]
-                if c == "D":
-                    dummies(int(tok[1:]))
-                elif c == "T":
-                    for h in range(2):
-                        transpose_bank(int(tok[1:]), h)
-                elif c == "Q":
-                    if tok[-1] == "h":
-                        quantise_h0(int(tok[1:-1]), 2)
-                    else:
-                        quantise_h0(int(tok[1:]))
-                elif c == "W":
-                    w_q["w2"] = prepare_w("w2")
-                elif c == "X":
-                    w_q["w1"] = prepare_w("w1")
-
-        def run_transposes(st):
-            if st == BIAS_AT:
-                bias_ps = spread_bias()
-            for n, g in enumerate(TR.get(st, (st + LAG_A,) if st + LAG_A < NG else ())):
-                for h in range(2):
-                    transpose_bank(g, h)
-                if st == BIAS_AT and n == 0:
-                    nc.scalar.copy(out=bias_f[:, 0 : U + 2], in_=bias_ps[:, 0 : U + 2])
-
-        do_head(HEAD if "X" in HEAD else HEAD.split()[0] + " X " + " ".join(HEAD.split()[1:]))
         for st in range(NSTEPS):
             first = GROUP * st - L2
             slots = [jj for jj in range(GROUP) if 0 <= first + jj < TILES]
-            plan = relu_plan(st)
-            if len(slots) < GROUP and st < NG:
-                plan = "GGGG"
+            plan = "GGGG" if first < 0 else relu_plan(st)
             g_slots = [jj for jj in slots if plan[jj] == "G"]
-            t_slots = [jj for jj in slots if plan[jj] != "G"]
             y = None
             if slots:
                 y = ypool.tile([P, GROUP * U], F32, name="y", tag="y")
             waiting = []
-            vwait = []
+            done = []
 
-            def tile_relus(upto):
+            def finished(s):
+                done.append(s)
+                n = 1 if st == NSTEPS - 1 else 2
+                base = s // n * n
+                if all(base + i in done for i in range(n)):
+                    store(y, first, base, base + n)
+
+            def scalar_relus(upto):
                 for s in [w for w in waiting if w <= upto]:
                     waiting.remove(s)
                     relu_scalar(y, s * U, (s + 1) * U)
-                    finished(y, first, s)
+                    finished(s)
 
             for jj in range(GROUP):
                 if st < NG:
                     stage1(st, jj)
-                    tile_relus(jj - RS_LAG)
-                if jj == TRPOS and st > 0:
-                    run_transposes(st)
+                    scalar_relus(jj - RS_LAG)
                 if jj in slots:
                     stage2(first + jj, y, jj)
-                    for s in vwait:
-                        relu_vector(y, s * U, (s + 1) * U)
-                        finished(y, first, s)
-                    vwait.clear()
-                    if plan[jj] == "V":
-                        vwait.append(jj)
-                    elif plan[jj] == "T":
+                    if plan[jj] == "T":
                         relu_gpsimd(y, jj * U, (jj + 1) * U)
-                        finished(y, first, jj)
-                    elif jj in t_slots:
+                        finished(jj)
+                    if plan[jj] == "S":
                         waiting.append(jj)
                     if st >= NG:
-                        tile_relus(jj)
-            if TRPOS == 4 or st == 0:
-                run_transposes(st)
-            tile_relus(GROUP)
-            for c in QORDER:
-                if c == "1" and st < NG:
-                    quantise_h1(st)
-                if c == "0":
-                    for g in Q0.get(st, (st + LAG_C,) if st + LAG_C < NG else ()):
-                        quantise_h0(g)
+                        scalar_relus(jj)
+            if st == 0:
+                bias_ps = spread_bias()
+                for g in range(HEAD_T, LAG_A + 1):
+                    if g > HEAD_T:
+                        dummies(WARM[2])
+                    for h in range(2):
+                        transpose_bank(g, h)
+                    if g == HEAD_T:
+                        nc.scalar.copy(out=bias_f[:, 0 : U + 2], in_=bias_ps[:, 0 : U + 2])
+            elif st + LAG_A < NG:
+                for h in range(2):
+                    transpose_bank(st + LAG_A, h)
+            scalar_relus(GROUP)
+            if st < NG:
+                quantise_h1(st)
+            if st + LAG_C < NG:
+                quantise_h0(st + LAG_C)
+            if st == 0:
+                for g in SORTED:
+                    for h in range(2):
+                        sort_words(g, h)
             if g_slots:
                 lo = g_slots[0] * U
-                relu_scalar(y, lo, lo + S_COLS)
-                lo += S_COLS
+                if st >= S_FROM:
+                    relu_scalar(y, lo, lo + S_COLS)
+                    lo += S_COLS
                 mine = y[:, lo : lo + V_COLS]
                 nc.vector.tensor_scalar(out=mine, in0=mine, scalar1=0.0, scalar2=None, op0=ALU.max)
                 relu_gpsimd(y, lo + V_COLS - LAP, (g_slots[-1] + 1) * U)

@@ -26,10 +26,10 @@ LAG_A = 3
 LAG_C = 2
 HEAD_T = 2
 SORTED = (4, 5)
-WARM = (12, 3, 2)
-V_COLS = 256
+WARM = (12, 2, 2)
+V_COLS = 128
 S_COLS = 256
-S_FROM = 3
+S_FROM = 2
 LAP = 8
 RS_LAG = 3
 NSTEPS = NG + (L2 + GROUP - 1) // GROUP

from contextlib import ExitStack

import concourse.masks as masks
import concourse.mybir as mybir

F32 = mybir.dt.float32
BF16 = mybir.dt.bfloat16
U32 = mybir.dt.uint32
U8 = mybir.dt.uint8
FP8X4 = mybir.dt.float8_e4m3fn_x4
ALU = mybir.AluOpType
ACT = mybir.ActivationFunctionType

P = 128
ROWS = 8192
U = 512
TILES = ROWS // P
GROUP = 4
NG = TILES // GROUP
GCOLS = GROUP * P
FLT_MAX = 3.4028234663852886e38
FLOPS = 2 * 2 * ROWS * U * U

L2 = 6
LAG_A = 3
LAG_C = 2
HEAD_T = 2
SORTED = (4, 5)
WARM = (12, 2, 2)
V_COLS = 128
S_COLS = 256
S_FROM = 2
LAP = 8
RS_LAG = 3
NSTEPS = NG + (L2 + GROUP - 1) // GROUP
LOADS = ["w1", (0, 2), (2, 4), (4, 8), "w2", (8, 12), (12, 16), (16, 20), (20, 24), (24, 28), (28, 32), (32, 48), (48, 64)]


def relu_plan(st):
    if st >= NG:
        return "SSSS"
    if st > NG - LAG_A:
        return "TTSS"
    return "SSGG" if st == NG - LAG_A else "GGGG"


def tile_sparsefactorisationdense_pa_t_kernel(tc, h0, k1, k2, m1, m2, scaling, bias, out):
    nc = tc.nc
    with ExitStack() as ctx:
        const = ctx.enter_context(tc.tile_pool(name="const", bufs=1))
        stage = ctx.enter_context(tc.tile_pool(name="stage", bufs=4))
        quant = ctx.enter_context(tc.tile_pool(name="quant", bufs=5))
        ypool = ctx.enter_context(tc.tile_pool(name="ypool", bufs=6))
        xpool = ctx.enter_context(tc.psum_pool(name="xpool", bufs=8))
        ctx.enter_context(tc.manual_schedule())

        h0v = h0.rearrange("(p j) k -> p (j k)", j=TILES)
        outv = out.rearrange("(p j) n -> p j n", j=TILES)

        brow = const.tile([P, U + 64], BF16, name="brow")
        ones = const.tile([P, P], BF16, name="ones")
        zeros = const.tile([P, U], BF16, name="zeros")
        nc.vector.memset(ones[:], 1.0)
        nc.vector.memset(zeros[:], 0.0)
        nc.vector.memset(brow[:], 0.0)
        warm = const.tile([P, 8], F32, name="warm")
        nc.vector.memset(warm[:], 0.0)
        nc.scalar.dma_start(out=brow[0:1, 0:U], in_=bias.rearrange("(o n) -> o n", o=1))
        nc.scalar.dma_start(out=brow[0:1, U : U + 1], in_=scaling.rearrange("(o n) -> o n", o=1))
        nc.scalar.activation(out=warm[:], in_=warm[:], func=ACT.Relu)
        ident = const.tile([P, P], F32, name="ident", align_bytes=256)
        masks.make_identity(nc, ident[:])

        w_sb = {}
        tile_src = {}
        for item in LOADS:
            if item in ("w1", "w2"):
                pair = []
                for name, src in (("k", k1 if item == "w1" else k2), ("m", m1 if item == "w1" else m2)):
                    t = const.tile([P, 4 * U], BF16, name=name + item)
                    w_sb[name + item] = t
                    pair.append((t, src.rearrange("(p j) c -> p (j c)", j=4)))
                for a in (0, 2 * U):
                    for t, v in pair:
                        nc.sync.dma_start(out=t[:, a : a + 2 * U], in_=v[:, a : a + 2 * U])
            else:
                t_a, t_b = item
                t = const.tile([P, (t_b - t_a) * U], BF16, name="h0t%d" % t_a, align_bytes=256)
                nc.sync.dma_start(out=t[:], in_=h0v[:, t_a * U : t_b * U])
                for i in range(t_a, t_b):
                    tile_src[i] = (t, i - t_a)

        dps = xpool.tile([P, U], F32, name="dps", tag="x")

        def dummies(n):
            for i in range(n):
                nc.tensor.matmul(out=dps[:], lhsT=ones[:], rhs=zeros[:], start=True, stop=True)

        bias_f = const.tile([P, U + 64], BF16, name="bias_f")

        def spread_bias():
            bias_ps = xpool.tile([P, 2 * U], BF16, name="bias_ps", tag="x")
            nc.tensor.matmul(out=bias_ps[:, 0:U], lhsT=ones[:], rhs=brow[:, 0:U], start=True, stop=True)
            nc.tensor.matmul(out=bias_ps[:, U : U + 64], lhsT=ones[:], rhs=brow[:, U : U + 64], start=True, stop=True)
            return bias_ps

        def quantise_into(codes, scales, src, a, b):
            nc.vector.quantize_mx(out=codes[:, a:b].bitcast(FP8X4), scales=scales[:, a:b], in_=src[:, 4 * a : 4 * b])

        def quantised(name, pool, width=GCOLS):
            codes = pool.tile([P, width], U32, name=name + "_c", tag=name + "_c", align_bytes=256)
            scales = pool.tile([P, width], U8, name=name + "_s", tag=name + "_s", align_bytes=256)
            return codes, scales

        def product(item, half):
            ks = w_sb["k" + item][:, half * 2 * U : (half + 1) * 2 * U]
            ms = w_sb["m" + item][:, half * 2 * U : (half + 1) * 2 * U]
            nc.vector.tensor_tensor(out=ks, in0=ks, in1=ms, op=ALU.mult)

        def quantise_w(item):
            kk = w_sb["k" + item]
            grouped = const.tile([P, 4 * U], BF16, name=item + "g", align_bytes=256)
            codes, scales = quantised(item, const, U)
            if item == "w1":
                dst = grouped[:].rearrange("p (s q t) -> p s q t", s=4, t=4)
                src = kk[:].rearrange("p (t q s) -> p s q t", t=4, s=4)
                for s in (0, 2):
                    nc.vector.tensor_copy(out=dst[:, s : s + 2], in_=src[:, s : s + 2])
            else:
                dst = grouped[:].rearrange("p (q t) -> p q t", t=4)
                src = kk[:].rearrange("p (t q) -> p q t", t=4)
                for s in (0, U // 2):
                    nc.vector.tensor_copy(out=dst[:, s : s + U // 2], in_=src[:, s : s + U // 2])
            for a in (0, U // 2):
                quantise_into(codes, scales, grouped, a, a + U // 2)
            return codes, scales

        g0_of, q0_of, g1_of, q1_of, w_q = {}, {}, {}, {}, {}
        sorted_of = {}

        def sort_words(g, h):
            src, i = tile_src[g * GROUP + 2 * h]
            t = const.tile([P, 2 * U], BF16, name="sorted%d_%d" % (g, h), align_bytes=256)
            nc.vector.tensor_copy(
                out=t[:].bitcast(F32).rearrange("p (j u w) -> p j u w", j=2, u=2),
                in_=src[:, i * U : (i + 2) * U].bitcast(F32).rearrange("p (j w u) -> p j u w", j=2, u=2),
            )
            sorted_of[g, h] = t

        def transpose_bank(g, h):
            if h == 0:
                g0_of[g] = stage.tile([P, 4 * GCOLS], BF16, name="g0", tag="g0", align_bytes=256)
            g0w = g0_of[g][:].bitcast(F32).rearrange("p (j r u) -> p j r u", j=GROUP, u=2)
            tp = xpool.tile([P, 2, 2, P], F32, name="tp", tag="x")
            for jj in range(2):
                src, i = tile_src[g * GROUP + 2 * h + jj]
                for u in range(2):
                    if g in SORTED:
                        w0 = (2 * jj + u) * P
                        words = sorted_of[g, h][:].bitcast(F32)[:, w0 : w0 + P]
                    else:
                        w0 = i * (U // 2)
                        words = src[:].bitcast(F32)[:, w0 + u : w0 + U // 2 : 2]
                    nc.tensor.transpose(tp[:, jj, u, :], words, ident[:])
            nc.scalar.copy(out=g0w[:, 2 * h : 2 * h + 2, :, :], in_=tp[:].rearrange("p j u r -> p j r u"))

        def quantise_h0(g, pieces=1):
            q0_of[g] = quantised("q0", quant)
            w = GCOLS // pieces
            for i in range(pieces):
                quantise_into(q0_of[g][0], q0_of[g][1], g0_of[g], i * w, (i + 1) * w)

        def stage1(g, jj):
            if jj == 0:
                g1_of[g] = stage.tile([P, 4 * GCOLS], BF16, name="g1", tag="g1", align_bytes=256)
            g1v = g1_of[g][:].rearrange("p (j r t) -> p j r t", j=GROUP, t=4)
            codes, scales = q0_of[g]
            w1c, w1s = w_q["w1"]
            s1 = xpool.tile([P, 4, P], F32, name="s1", tag="x")
            cols = slice(jj * P, (jj + 1) * P)
            for t in range(4):
                wcols = slice(t * P, (t + 1) * P)
                nc.tensor.matmul_mx(
                    out=s1[:, t, :],
                    lhsT=w1c[:, wcols].bitcast(FP8X4),
                    lhsT_scale=w1s[:, wcols],
                    rhs=codes[:, cols].bitcast(FP8X4),
                    rhs_scale=scales[:, cols],
                    start=True,
                    stop=True,
                )
            nc.scalar.copy(out=g1v[:, jj, :, :], in_=s1[:].rearrange("p t r -> p r t"))

        def quantise_h1(g):
            q1_of[g] = quantised("q1", quant)
            quantise_into(q1_of[g][0], q1_of[g][1], g1_of[g], 0, GCOLS)

        def stage2(tile_no, y, slot):
            codes, scales = q1_of[tile_no // GROUP]
            w2c, w2s = w_q["w2"]
            cols = slice((tile_no % GROUP) * P, (tile_no % GROUP + 1) * P)
            s2 = xpool.tile([P, U], F32, name="s2", tag="x")
            nc.tensor.matmul_mx(
                out=s2[:],
                lhsT=codes[:, cols].bitcast(FP8X4),
                lhsT_scale=scales[:, cols],
                rhs=w2c[:].bitcast(FP8X4),
                rhs_scale=w2s[:],
                start=True,
                stop=True,
            )
            nc.vector.scalar_tensor_tensor(
                out=y[:, slot * U : (slot + 1) * U],
                in0=s2[:],
                scalar=bias_f[:, U : U + 1],
                in1=bias_f[:, 0:U],
                op0=ALU.mult,
                op1=ALU.add,
            )

        def relu_scalar(y, a, b):
            nc.scalar.activation(out=y[:, a:b], in_=y[:, a:b], func=ACT.Relu)

        def relu_gpsimd(y, a, b):
            nc.gpsimd.tensor_scalar(out=y[:, a:b], in0=y[:, a:b], scalar1=FLT_MAX, scalar2=0.0, op0=ALU.min, op1=ALU.max)

        def store(y, first_tile, slot_a, slot_b):
            nc.sync.dma_start(
                out=outv[:, first_tile + slot_a : first_tile + slot_b, :],
                in_=y[:, slot_a * U : slot_b * U].rearrange("p (j n) -> p j n", n=U),
            )

        dummies(WARM[0])
        for half in range(2):
            product("w1", half)
        w_q["w1"] = quantise_w("w1")
        for g in range(HEAD_T):
            for h in range(2):
                transpose_bank(g, h)
            if g == 0:
                dummies(WARM[1])
        quantise_h0(0, 2)
        product("w2", 0)
        quantise_h0(1)
        product("w2", 1)
        w_q["w2"] = quantise_w("w2")

        for st in range(NSTEPS):
            first = GROUP * st - L2
            slots = [jj for jj in range(GROUP) if 0 <= first + jj < TILES]
            plan = "GGGG" if first < 0 else relu_plan(st)
            g_slots = [jj for jj in slots if plan[jj] == "G"]
            y = None
            if slots:
                y = ypool.tile([P, GROUP * U], F32, name="y", tag="y")
            waiting = []
            done = []

            def finished(s):
                done.append(s)
                n = 1 if st == NSTEPS - 1 else 2
                base = s // n * n
                if all(base + i in done for i in range(n)):
                    store(y, first, base, base + n)

            def scalar_relus(upto):
                for s in [w for w in waiting if w <= upto]:
                    waiting.remove(s)
                    relu_scalar(y, s * U, (s + 1) * U)
                    finished(s)

            for jj in range(GROUP):
                if st < NG:
                    stage1(st, jj)
                    scalar_relus(jj - RS_LAG)
                if jj in slots:
                    stage2(first + jj, y, jj)
                    if plan[jj] == "T":
                        relu_gpsimd(y, jj * U, (jj + 1) * U)
                        finished(jj)
                    if plan[jj] == "S":
                        waiting.append(jj)
                    if st >= NG:
                        scalar_relus(jj)
            if st == 0:
                bias_ps = spread_bias()
                for g in range(HEAD_T, LAG_A + 1):
                    if g > HEAD_T:
                        dummies(WARM[2])
                    for h in range(2):
                        transpose_bank(g, h)
                    if g == HEAD_T:
                        nc.scalar.copy(out=bias_f[:, 0 : U + 2], in_=bias_ps[:, 0 : U + 2])
            elif st + LAG_A < NG:
                for h in range(2):
                    transpose_bank(st + LAG_A, h)
            scalar_relus(GROUP)
            if st < NG:
                quantise_h1(st)
            if st + LAG_C < NG:
                quantise_h0(st + LAG_C)
            if st == 0:
                for g in SORTED:
                    for h in range(2):
                        sort_words(g, h)
            if g_slots:
                lo = g_slots[0] * U
                if st >= S_FROM:
                    relu_scalar(y, lo, lo + S_COLS)
                    lo += S_COLS
                mine = y[:, lo : lo + V_COLS]
                nc.vector.tensor_scalar(out=mine, in0=mine, scalar1=0.0, scalar2=None, op0=ALU.max)
                relu_gpsimd(y, lo + V_COLS - LAP, (g_slots[-1] + 1) * U)
                store(y, first, g_slots[0], g_slots[-1] + 1)
